import numpy as np
import ml_dtypes


def mxq(x, axis, fmt="e4m3"):
    dtype, down = {"e4m3": (ml_dtypes.float8_e4m3fn, 7), "e5m2": (ml_dtypes.float8_e5m2, 14)}[fmt]
    v = np.moveaxis(np.asarray(x, np.float32).astype(ml_dtypes.bfloat16).astype(np.float64), axis, -1)
    blocks = v.reshape(v.shape[:-1] + (-1, 32))
    amax = np.abs(blocks).max(-1, keepdims=True)
    byte = np.maximum(np.where(amax > 0, np.frexp(amax)[1] - 1 + 127, 0) - down, 1)
    scale = np.exp2(byte - 127.0)
    codes = (blocks / scale).astype(np.float32).astype(dtype).astype(np.float64)
    return np.moveaxis((codes * scale).reshape(v.shape), -1, axis)


WIDE = False


def mx_kscale(k):
    if not WIDE:
        return np.ones(k)
    levels = np.array([10, -10, 5, -5, 0])
    a = np.random.permutation(np.resize(levels, k // 512 * 4)).reshape(k // 512, 4)
    idx = np.arange(k)
    return np.exp2(a[idx // 512, idx % 128 // 32])


BF16 = ml_dtypes.bfloat16


def bf(x):
    return np.asarray(x, np.float32).astype(BF16)


def f64(x):
    return np.asarray(x).astype(np.float64)


B, S, HID, QK, H, C = 1, 4096, 256, 256, 2, 512
DK, DV = QK // H, HID // H
GFAST, GSLOW = 0.96875, 0.99609375


def setup_inputs():
    s = mx_kscale(S)
    lg = np.linspace(np.log(1.0 - GFAST), np.log(1.0 - GSLOW), H) + 0.3 * (np.random.random_sample(H) - 0.5)
    return {"q": bf(np.random.standard_normal((B, H, S, DK)) / DK ** 0.25),
            "k": bf(np.random.standard_normal((B, H, S, DK)) / DK ** 0.25 * s[:, None]),
            "v": bf(np.random.standard_normal((B, H, S, DV)) * 0.5 / s[:, None]),
            "gamma": bf(1.0 - np.exp(lg))}


def reference(q, k, v, gamma):
    q, k, g = f64(q), f64(k), f64(gamma)
    vq = mxq(f64(v), 2, "e4m3")
    idx = f64(np.arange(S))
    ret = np.zeros((B, H, S, DV))
    for i in range(S // C):
        r0, e = i * C, (i + 1) * C
        diff = idx[r0:e, None] - idx[None, :e]
        expn = np.maximum(diff, 0.0)
        dmask = np.where(diff >= 0, g[:, None, None] ** expn, 0.0)
        sc = (q[:, :, r0:e] @ k[:, :, :e].transpose(0, 1, 3, 2)) * dmask[None]
        ret[:, :, r0:e] = mxq(sc, 3, "e4m3") @ vq[:, :, :e]
    return ret

@@ -1,0 +1,214 @@
+from contextlib import ExitStack
+
+import concourse.mybir as mybir
+from concourse.masks import make_identity
+
+F32 = mybir.dt.float32
+BF16 = mybir.dt.bfloat16
+U32 = mybir.dt.uint32
+U8 = mybir.dt.uint8
+FP8X4 = mybir.dt.float8_e4m3fn_x4
+ALU = mybir.AluOpType
+ACT = mybir.ActivationFunctionType
+
+P = 128
+PACK = 4
+GROUP = P * PACK
+HEADS = 2
+CHUNKS = 8
+TILES = 4
+QUAD = 4
+NEAR = TILES + 1
+FAR = TILES * (CHUNKS - 1)
+LN_TERMS = 8
+
+FLOPS = 2 * 2 * P * HEADS * GROUP * GROUP * (CHUNKS * (CHUNKS + 1) // 2)
+
+
+def tile_multiscaleretention_pa_t_kernel(tc, q, k, v, gamma, out):
+    nc = tc.nc
+    with ExitStack() as ctx:
+        consts = ctx.enter_context(tc.tile_pool(name="consts", bufs=1))
+        raw = ctx.enter_context(tc.tile_pool(name="raw", bufs=1))
+        keep = ctx.enter_context(tc.tile_pool(name="keep", bufs=1))
+        stage = ctx.enter_context(tc.tile_pool(name="stage", bufs=2))
+        packed = ctx.enter_context(tc.tile_pool(name="packed", bufs=3))
+        results = ctx.enter_context(tc.tile_pool(name="results", bufs=3))
+        psum_turn = ctx.enter_context(tc.psum_pool(name="psum_turn", bufs=1))
+        psum_first = ctx.enter_context(tc.psum_pool(name="psum_first", bufs=2))
+        psum_rest = ctx.enter_context(tc.psum_pool(name="psum_rest", bufs=3))
+        psum_out = ctx.enter_context(tc.psum_pool(name="psum_out", bufs=2))
+        ctx.enter_context(tc.manual_schedule())
+
+        gamma_bf = consts.tile([P, HEADS], BF16)
+        nc.sync.dma_start(out=gamma_bf[:], in_=gamma.partition_broadcast(P))
+        k_raw, q_raw, v_raw = {}, {}, {}
+        for h in range(HEADS):
+            for i in range(CHUNKS):
+                rows = slice(i * GROUP, (i + 1) * GROUP)
+                k_raw[h, i] = raw.tile([P, PACK, P], BF16, name="k_raw_%d_%d" % (h, i))
+                q_raw[h, i] = raw.tile([P, TILES, P], BF16, name="q_raw_%d_%d" % (h, i))
+                v_raw[h, i] = raw.tile([P, PACK, P], BF16, name="v_raw_%d_%d" % (h, i))
+                nc.sync.dma_start(out=k_raw[h, i][:], in_=k[0, h, rows, :].rearrange("(p t) d -> p t d", t=PACK))
+                nc.sync.dma_start(out=q_raw[h, i][:], in_=q[0, h, rows, :].rearrange("(c p) d -> p c d", p=P))
+                nc.sync.dma_start(out=v_raw[h, i][:], in_=v[0, h, rows, :].rearrange("(p t) d -> p t d", t=PACK))
+
+        identity = consts.tile([P, P], BF16)
+        make_identity(nc, identity[:])
+        offsets = consts.tile([P, P, PACK], F32)
+        nc.gpsimd.iota(offsets[:], pattern=[[1, P], [-1, PACK]], base=0, channel_multiplier=0,
+                       allow_small_or_imprecise_dtypes=True)
+        near_steps = consts.tile([P, NEAR], F32)
+        nc.gpsimd.iota(near_steps[:], pattern=[[P, NEAR]], base=0, channel_multiplier=-PACK,
+                       allow_small_or_imprecise_dtypes=True)
+        far_steps = consts.tile([P, FAR], F32)
+        nc.gpsimd.iota(far_steps[:], pattern=[[P, FAR]], base=0, channel_multiplier=0,
+                       allow_small_or_imprecise_dtypes=True)
+        zero = consts.tile([P, 1], F32)
+        warm = consts.tile([P, 1], F32)
+        nc.vector.memset(zero[:], 0.0)
+        nc.scalar.activation(out=warm[:], in_=zero[:], func=ACT.Exp)
+
+        kq_turned, v_codes, v_scales, v_grouped = {}, {}, {}, {}
+
+        def turn_chunk(h, i):
+            turned = psum_turn.tile([P, PACK + TILES, P], BF16)
+            for t in range(PACK):
+                nc.tensor.transpose(turned[:, t, :], k_raw[h, i][:, t, :], identity[:])
+            for c in range(TILES):
+                nc.tensor.transpose(turned[:, PACK + c, :], q_raw[h, i][:, c, :], identity[:])
+            kq_turned[h, i] = keep.tile([P, PACK + TILES, P], BF16, name="kq_turned_%d_%d" % (h, i))
+            nc.scalar.copy(out=kq_turned[h, i][:], in_=turned[:])
+            v_grouped[h, i] = stage.tile([P, P, PACK], BF16, name="v_grouped", align_bytes=64)
+            nc.scalar.copy(out=v_grouped[h, i][:], in_=v_raw[h, i][:].rearrange("p t d -> p d t"))
+
+        def quantise_values(h, i):
+            v_codes[h, i] = keep.tile([P, P], U32, name="v_codes_%d_%d" % (h, i), align_bytes=64)
+            v_scales[h, i] = keep.tile([P, P], U8, name="v_scales_%d_%d" % (h, i), align_bytes=64)
+            nc.vector.quantize_mx(
+                out=v_codes[h, i][:].bitcast(FP8X4),
+                scales=v_scales[h, i][:],
+                in_=v_grouped[h, i][:].rearrange("p d t -> p (d t)"),
+            )
+
+        turn_chunk(0, 0)
+
+        x = consts.tile([P, HEADS], F32)
+        x_sq = consts.tile([P, HEADS], F32)
+        tail = consts.tile([P, HEADS], F32)
+        head_terms = consts.tile([P, HEADS], F32)
+        ln_gamma = consts.tile([P, HEADS], F32)
+        nc.vector.tensor_scalar(out=x[:], in0=gamma_bf[:], scalar1=-1.0, scalar2=1.0, op0=ALU.mult, op1=ALU.add)
+        nc.vector.tensor_scalar(out=tail[:], in0=x[:], scalar1=1.0 / LN_TERMS, scalar2=None, op0=ALU.mult)
+        for term in range(LN_TERMS - 1, 2, -1):
+            nc.vector.scalar_tensor_tensor(out=tail[:], in0=tail[:], scalar=1.0 / term, in1=x[:],
+                                           op0=ALU.add, op1=ALU.mult)
+        nc.vector.tensor_tensor(out=x_sq[:], in0=x[:], in1=x[:], op=ALU.mult)
+        nc.vector.tensor_tensor(out=tail[:], in0=tail[:], in1=x_sq[:], op=ALU.mult)
+        nc.vector.scalar_tensor_tensor(out=head_terms[:], in0=x_sq[:], scalar=0.5, in1=x[:],
+                                       op0=ALU.mult, op1=ALU.add)
+        nc.vector.scalar_tensor_tensor(out=ln_gamma[:], in0=head_terms[:], scalar=-1.0, in1=tail[:],
+                                       op0=ALU.mult, op1=ALU.subtract)
+
+        near_bias, far, near = {}, {}, {}
+        for h in range(HEADS):
+            ln_h = ln_gamma[:, h : h + 1]
+            near_bias[h] = consts.tile([P, NEAR], F32, name="near_bias_%d" % h)
+            far[h] = consts.tile([P, FAR], F32, name="far_%d" % h)
+            near[h] = consts.tile([P, NEAR, P, PACK], F32, name="near_%d" % h)
+            nc.vector.tensor_scalar(out=near_bias[h][:], in0=near_steps[:], scalar1=ln_h, scalar2=None, op0=ALU.mult)
+            nc.scalar.activation(out=far[h][:], in_=far_steps[:], func=ACT.Exp, scale=ln_h)
+
+        def near_table(h, s):
+            nc.scalar.activation(out=near[h][:, s], in_=offsets[:], func=ACT.Exp,
+                                 scale=ln_gamma[:, h : h + 1], bias=near_bias[h][:, s : s + 1])
+            if s < TILES:
+                nc.gpsimd.affine_select(out=near[h][:, s], in_=near[h][:, s], pattern=[[1, P], [-1, PACK]],
+                                        compare_op=ALU.is_ge, fill=0.0, base=P * s, channel_multiplier=-PACK)
+
+        for s in range(NEAR):
+            near_table(0, s)
+
+        def mask_of(h, i, c, g):
+            if g == i:
+                return near[h][:, c], far[h][:, 0:1]
+            j = TILES * (i - g - 1) + c
+            return near[h][:, TILES], far[h][:, j : j + 1]
+
+        items = [(h, i, c, g) for h in range(HEADS) for i in range(CHUNKS) for c in range(TILES) for g in range(i + 1)]
+        quads = [items[a : a + QUAD] for a in range(0, len(items), QUAD)]
+        banks, scaled, grouped, codes, scales, sums = {}, {}, {}, {}, {}, {}
+
+        def scores(n, slot):
+            h, i, c, g = quads[n][slot]
+            pool = psum_first if slot == 0 else psum_rest
+            bank = pool.tile([P, PACK, P], F32)
+            for t in range(PACK):
+                nc.tensor.matmul(out=bank[:, t, :], lhsT=kq_turned[h, g][:, t, :],
+                                 rhs=kq_turned[h, i][:, PACK + c, :], start=True, stop=True)
+            banks[n, slot] = bank
+
+        def scale_first(n):
+            table, number = mask_of(*quads[n][0])
+            scaled[n] = stage.tile([P, P, PACK], F32, name="scaled")
+            nc.scalar.activation(out=scaled[n][:], in_=banks[n, 0][:].rearrange("p t n -> p n t"),
+                                 func=ACT.Copy, scale=number)
+
+        def mask_first(n):
+            table, number = mask_of(*quads[n][0])
+            grouped[n] = stage.tile([P, QUAD, P, PACK], BF16, name="grouped", align_bytes=64)
+            nc.gpsimd.tensor_tensor(out=grouped[n][:, 0], in0=scaled[n][:], in1=table, op=ALU.mult)
+
+        def mask_rest(n):
+            for slot in range(1, QUAD):
+                table, number = mask_of(*quads[n][slot])
+                nc.vector.scalar_tensor_tensor(out=grouped[n][:, slot], in0=banks[n, slot][:].rearrange("p t n -> p n t"),
+                                               scalar=number, in1=table, op0=ALU.mult, op1=ALU.mult)
+
+        def quantise_scores(n):
+            codes[n] = packed.tile([P, QUAD * P], U32, name="codes", align_bytes=64)
+            scales[n] = packed.tile([P, QUAD * P], U8, name="scales", align_bytes=64)
+            nc.vector.quantize_mx(out=codes[n][:].bitcast(FP8X4), scales=scales[n][:],
+                                  in_=grouped[n][:].rearrange("p s n t -> p (s n t)"))
+
+        def attend(n):
+            for slot in range(QUAD):
+                h, i, c, g = quads[n][slot]
+                if c == 0 and g == 0:
+                    sums[h, i] = psum_out.tile([P, TILES, P], F32, name="sums")
+                cols = slice(slot * P, (slot + 1) * P)
+                nc.tensor.matmul_mx(out=sums[h, i][:, c, :],
+                                    lhsT=codes[n][:, cols].bitcast(FP8X4), lhsT_scale=scales[n][:, cols],
+                                    rhs=v_codes[h, g][:].bitcast(FP8X4), rhs_scale=v_scales[h, g][:],
+                                    start=(g == 0), stop=(g == i))
+                if c == TILES - 1 and g == i:
+                    result = results.tile([P, TILES, P], F32)
+                    nc.scalar.copy(out=result[:], in_=sums[h, i][:])
+                    rows = slice(i * GROUP, (i + 1) * GROUP)
+                    nc.sync.dma_start(out=out[0, h, rows, :].rearrange("(c p) d -> p c d", p=P), in_=result[:])
+
+        turned_last = (0, 0)
+        for n in range(-1, len(quads) + 2):
+            if 0 <= n - 2:
+                attend(n - 2)
+            if 0 <= n < len(quads):
+                mask_rest(n)
+            if n + 1 < len(quads):
+                for slot in range(QUAD):
+                    scores(n + 1, slot)
+                scale_first(n + 1)
+            if 0 <= n - 1 < len(quads):
+                quantise_scores(n - 1)
+            if turned_last is not None:
+                quantise_values(*turned_last)
+                turned_last = None
+            if n + 1 < len(quads):
+                mask_first(n + 1)
+            if n + 2 < len(quads):
+                h, i, c, g = quads[n + 2][0]
+                if c == 0 and g == 0:
+                    turn_chunk(h, i)
+                    turned_last = (h, i)
+                    s = i - (CHUNKS - NEAR)
+                    if h + 1 < HEADS and s >= 0:
+                        near_table(h + 1, s)

@@ -159,11 +159,10 @@ def tile_multiscaleretention_pa_t_kernel(tc, q, k, v, gamma, out):
             grouped[n] = stage.tile([P, QUAD, P, PACK], BF16, name="grouped", align_bytes=64)
             nc.gpsimd.tensor_tensor(out=grouped[n][:, 0], in0=scaled[n][:], in1=table, op=ALU.mult)
 
-        def mask_rest(n):
-            for slot in range(1, QUAD):
-                table, number = mask_of(*quads[n][slot])
-                nc.vector.scalar_tensor_tensor(out=grouped[n][:, slot], in0=banks[n, slot][:].rearrange("p t n -> p n t"),
-                                               scalar=number, in1=table, op0=ALU.mult, op1=ALU.mult)
+        def mask_rest(n, slot):
+            table, number = mask_of(*quads[n][slot])
+            nc.vector.scalar_tensor_tensor(out=grouped[n][:, slot], in0=banks[n, slot][:].rearrange("p t n -> p n t"),
+                                           scalar=number, in1=table, op0=ALU.mult, op1=ALU.mult)
 
         def quantise_scores(n):
             codes[n] = packed.tile([P, QUAD * P], U32, name="codes", align_bytes=64)
@@ -187,25 +186,31 @@ def tile_multiscaleretention_pa_t_kernel(tc, q, k, v, gamma, out):
                     rows = slice(i * GROUP, (i + 1) * GROUP)
                     nc.sync.dma_start(out=out[0, h, rows, :].rearrange("(c p) d -> p c d", p=P), in_=result[:])
 
+        last = len(quads)
         turned_last = (0, 0)
-        for n in range(-1, len(quads) + 2):
+        for n in range(-2, last + 2):
             if 0 <= n - 2:
                 attend(n - 2)
-            if 0 <= n < len(quads):
-                mask_rest(n)
-            if n + 1 < len(quads):
-                for slot in range(QUAD):
-                    scores(n + 1, slot)
-                scale_first(n + 1)
-            if 0 <= n - 1 < len(quads):
+            if 0 <= n < last:
+                mask_rest(n, 1)
+            if 0 <= n - 1 < last:
                 quantise_scores(n - 1)
+            if 0 <= n + 1 < last:
+                mask_first(n + 1)
+            if 0 <= n < last:
+                mask_rest(n, 2)
+                mask_rest(n, 3)
+            if n + 2 < last:
+                scores(n + 2, 0)
+                scale_first(n + 2)
+            if 0 <= n + 1 < last:
+                for slot in range(1, QUAD):
+                    scores(n + 1, slot)
             if turned_last is not None:
                 quantise_values(*turned_last)
                 turned_last = None
-            if n + 1 < len(quads):
-                mask_first(n + 1)
-            if n + 2 < len(quads):
-                h, i, c, g = quads[n + 2][0]
+            if n + 3 < last:
+                h, i, c, g = quads[n + 3][0]
                 if c == 0 and g == 0:
                     turn_chunk(h, i)
                     turned_last = (h, i)

@@ -17,10 +17,14 @@ GROUP = P * PACK
 HEADS = 2
 CHUNKS = 8
 TILES = 4
-QUAD = 4
+UNIT = 8
+HELPED = 2
+DIRECT = UNIT - HELPED - 1
+DIRECT_BANKS = 3
 NEAR = TILES + 1
 FAR = TILES * (CHUNKS - 1)
 LN_TERMS = 8
+SHIFT = 30.0
 
 FLOPS = 2 * 2 * P * HEADS * GROUP * GROUP * (CHUNKS * (CHUNKS + 1) // 2)
 
@@ -34,9 +38,8 @@ def tile_multiscaleretention_pa_t_kernel(tc, q, k, v, gamma, out):
         stage = ctx.enter_context(tc.tile_pool(name="stage", bufs=2))
         packed = ctx.enter_context(tc.tile_pool(name="packed", bufs=3))
         results = ctx.enter_context(tc.tile_pool(name="results", bufs=3))
-        psum_turn = ctx.enter_context(tc.psum_pool(name="psum_turn", bufs=1))
-        psum_first = ctx.enter_context(tc.psum_pool(name="psum_first", bufs=2))
-        psum_rest = ctx.enter_context(tc.psum_pool(name="psum_rest", bufs=3))
+        psum_vector = ctx.enter_context(tc.psum_pool(name="psum_vector", bufs=DIRECT_BANKS))
+        psum_scalar = ctx.enter_context(tc.psum_pool(name="psum_scalar", bufs=3))
         psum_out = ctx.enter_context(tc.psum_pool(name="psum_out", bufs=2))
         ctx.enter_context(tc.manual_schedule())
 
@@ -45,40 +48,49 @@ def tile_multiscaleretention_pa_t_kernel(tc, q, k, v, gamma, out):
         k_raw, q_raw, v_raw = {}, {}, {}
         for h in range(HEADS):
             for i in range(CHUNKS):
-                rows = slice(i * GROUP, (i + 1) * GROUP)
+                rows_of_chunk = slice(i * GROUP, (i + 1) * GROUP)
                 k_raw[h, i] = raw.tile([P, PACK, P], BF16, name="k_raw_%d_%d" % (h, i))
                 q_raw[h, i] = raw.tile([P, TILES, P], BF16, name="q_raw_%d_%d" % (h, i))
                 v_raw[h, i] = raw.tile([P, PACK, P], BF16, name="v_raw_%d_%d" % (h, i))
-                nc.sync.dma_start(out=k_raw[h, i][:], in_=k[0, h, rows, :].rearrange("(p t) d -> p t d", t=PACK))
-                nc.sync.dma_start(out=q_raw[h, i][:], in_=q[0, h, rows, :].rearrange("(c p) d -> p c d", p=P))
-                nc.sync.dma_start(out=v_raw[h, i][:], in_=v[0, h, rows, :].rearrange("(p t) d -> p t d", t=PACK))
+                nc.sync.dma_start(out=k_raw[h, i][:], in_=k[0, h, rows_of_chunk, :].rearrange("(p t) d -> p t d", t=PACK))
+                nc.sync.dma_start(out=q_raw[h, i][:], in_=q[0, h, rows_of_chunk, :].rearrange("(c p) d -> p c d", p=P))
+                nc.sync.dma_start(out=v_raw[h, i][:], in_=v[0, h, rows_of_chunk, :].rearrange("(p t) d -> p t d", t=PACK))
 
         identity = consts.tile([P, P], BF16)
         make_identity(nc, identity[:])
-        offsets = consts.tile([P, P, PACK], F32)
-        nc.gpsimd.iota(offsets[:], pattern=[[1, P], [-1, PACK]], base=0, channel_multiplier=0,
-                       allow_small_or_imprecise_dtypes=True)
-        near_steps = consts.tile([P, NEAR], F32)
-        nc.gpsimd.iota(near_steps[:], pattern=[[P, NEAR]], base=0, channel_multiplier=-PACK,
-                       allow_small_or_imprecise_dtypes=True)
-        far_steps = consts.tile([P, FAR], F32)
-        nc.gpsimd.iota(far_steps[:], pattern=[[P, FAR]], base=0, channel_multiplier=0,
-                       allow_small_or_imprecise_dtypes=True)
-        zero = consts.tile([P, 1], F32)
+
+        def count(name, width, pattern, base, per_partition):
+            numbers = consts.tile([P] + width, F32, name=name)
+            nc.gpsimd.iota(numbers[:], pattern=pattern, base=base, channel_multiplier=per_partition,
+                           allow_small_or_imprecise_dtypes=True)
+            return numbers
+
+        offsets = count("offsets", [P, PACK], [[1, P], [-1, PACK]], 0, 0)
+        near_steps = count("near_steps", [NEAR], [[P, NEAR]], 0, -PACK)
+        far_steps = count("far_steps", [FAR], [[P, FAR]], 0, 0)
+        row_steps = count("row_steps", [PACK], [[-1, PACK]], PACK - 1, 1)
+        col_steps = count("col_steps", [1], [[0, 1]], GROUP - PACK + 1, -PACK)
+        identity_f32 = consts.tile([P, P], F32)
+        make_identity(nc, identity_f32[:])
+        shift_up = consts.tile([P, 1], F32)
+        shift_down = consts.tile([P, 1], F32)
+        nc.vector.memset(shift_up[:], SHIFT)
+        nc.vector.memset(shift_down[:], -SHIFT)
         warm = consts.tile([P, 1], F32)
-        nc.vector.memset(zero[:], 0.0)
-        nc.scalar.activation(out=warm[:], in_=zero[:], func=ACT.Exp)
+        nc.scalar.activation(out=warm[:], in_=shift_down[:], func=ACT.Exp)
 
         kq_turned, v_codes, v_scales, v_grouped = {}, {}, {}, {}
 
         def turn_chunk(h, i):
-            turned = psum_turn.tile([P, PACK + TILES, P], BF16)
+            turned = psum_scalar.tile([P, PACK + TILES, P], BF16, name="turned", tag="for_scalar")
             for t in range(PACK):
                 nc.tensor.transpose(turned[:, t, :], k_raw[h, i][:, t, :], identity[:])
             for c in range(TILES):
                 nc.tensor.transpose(turned[:, PACK + c, :], q_raw[h, i][:, c, :], identity[:])
             kq_turned[h, i] = keep.tile([P, PACK + TILES, P], BF16, name="kq_turned_%d_%d" % (h, i))
             nc.scalar.copy(out=kq_turned[h, i][:], in_=turned[:])
+
+        def regroup_values(h, i):
             v_grouped[h, i] = stage.tile([P, P, PACK], BF16, name="v_grouped", align_bytes=64)
             nc.scalar.copy(out=v_grouped[h, i][:], in_=v_raw[h, i][:].rearrange("p t d -> p d t"))
 
@@ -90,8 +102,6 @@ def tile_multiscaleretention_pa_t_kernel(tc, q, k, v, gamma, out):
                 scales=v_scales[h, i][:],
                 in_=v_grouped[h, i][:].rearrange("p d t -> p (d t)"),
             )
-
-        turn_chunk(0, 0)
 
         x = consts.tile([P, HEADS], F32)
         x_sq = consts.tile([P, HEADS], F32)
@@ -110,14 +120,27 @@ def tile_multiscaleretention_pa_t_kernel(tc, q, k, v, gamma, out):
         nc.vector.scalar_tensor_tensor(out=ln_gamma[:], in0=head_terms[:], scalar=-1.0, in1=tail[:],
                                        op0=ALU.mult, op1=ALU.subtract)
 
-        near_bias, far, near = {}, {}, {}
+        near_bias, col_bias, near, far, row_fac, col_fac = {}, {}, {}, {}, {}, {}
         for h in range(HEADS):
             ln_h = ln_gamma[:, h : h + 1]
             near_bias[h] = consts.tile([P, NEAR], F32, name="near_bias_%d" % h)
-            far[h] = consts.tile([P, FAR], F32, name="far_%d" % h)
+            col_bias[h] = consts.tile([P, 1], F32, name="col_bias_%d" % h)
             near[h] = consts.tile([P, NEAR, P, PACK], F32, name="near_%d" % h)
-            nc.vector.tensor_scalar(out=near_bias[h][:], in0=near_steps[:], scalar1=ln_h, scalar2=None, op0=ALU.mult)
-            nc.scalar.activation(out=far[h][:], in_=far_steps[:], func=ACT.Exp, scale=ln_h)
+            far[h] = consts.tile([P, FAR], F32, name="far_%d" % h)
+            row_fac[h] = consts.tile([P, PACK], F32, name="row_fac_%d" % h)
+            col_fac[h] = consts.tile([P, FAR], F32, name="col_fac_%d" % h)
+            nc.vector.tensor_scalar(out=near_bias[h][:, 0:TILES], in0=near_steps[:, 0:TILES], scalar1=ln_h,
+                                    scalar2=None, op0=ALU.mult)
+            nc.vector.tensor_scalar(out=near_bias[h][:, TILES:NEAR], in0=near_steps[:, TILES:NEAR], scalar1=ln_h,
+                                    scalar2=-SHIFT, op0=ALU.mult, op1=ALU.add)
+            nc.vector.tensor_scalar(out=col_bias[h][:], in0=col_steps[:], scalar1=ln_h,
+                                    scalar2=SHIFT, op0=ALU.mult, op1=ALU.add)
+
+        def small_factors(h):
+            ln_h = ln_gamma[:, h : h + 1]
+            nc.scalar.activation(out=far[h][:], in_=far_steps[:], func=ACT.Exp, scale=ln_h, bias=shift_up[:])
+            nc.scalar.activation(out=row_fac[h][:], in_=row_steps[:], func=ACT.Exp, scale=ln_h, bias=shift_down[:])
+            nc.scalar.activation(out=col_fac[h][:], in_=far_steps[:], func=ACT.Exp, scale=ln_h, bias=col_bias[h][:])
 
         def near_table(h, s):
             nc.scalar.activation(out=near[h][:, s], in_=offsets[:], func=ACT.Exp,
@@ -126,94 +149,156 @@ def tile_multiscaleretention_pa_t_kernel(tc, q, k, v, gamma, out):
                 nc.gpsimd.affine_select(out=near[h][:, s], in_=near[h][:, s], pattern=[[1, P], [-1, PACK]],
                                         compare_op=ALU.is_ge, fill=0.0, base=P * s, channel_multiplier=-PACK)
 
-        for s in range(NEAR):
-            near_table(0, s)
+        def far_index(i, c, g):
+            return TILES * (i - g - 1) + c
 
-        def mask_of(h, i, c, g):
+        def table_and_number(h, i, c, g):
             if g == i:
-                return near[h][:, c], far[h][:, 0:1]
-            j = TILES * (i - g - 1) + c
+                return near[h][:, c], 1.0
+            j = far_index(i, c, g)
             return near[h][:, TILES], far[h][:, j : j + 1]
 
         items = [(h, i, c, g) for h in range(HEADS) for i in range(CHUNKS) for c in range(TILES) for g in range(i + 1)]
-        quads = [items[a : a + QUAD] for a in range(0, len(items), QUAD)]
-        banks, scaled, grouped, codes, scales, sums = {}, {}, {}, {}, {}, {}
+        units = [items[a : a + UNIT] for a in range(0, len(items), UNIT)]
+        last = len(units)
 
-        def scores(n, slot):
-            h, i, c, g = quads[n][slot]
-            pool = psum_first if slot == 0 else psum_rest
-            bank = pool.tile([P, PACK, P], F32)
+        def live(n):
+            return 0 <= n < last
+
+        def detour_slot(n):
+            return [slot for slot in range(UNIT) if units[n][slot][3] < units[n][slot][1]][0]
+
+        def other_slots(n):
+            return [slot for slot in range(UNIT) if slot != detour_slot(n)]
+
+        def direct_slot(n, r):
+            return other_slots(n)[r]
+
+        def helped_slot(n, r):
+            return other_slots(n)[DIRECT + r]
+
+        banks, scaled, wide, rows, back, grouped, codes, scales, sums = {}, {}, {}, {}, {}, {}, {}, {}, {}
+
+        def keys_on_partitions(pool, tag, h, i, c, g):
+            bank = pool.tile([P, PACK, P], F32, name="bank", tag=tag)
             for t in range(PACK):
                 nc.tensor.matmul(out=bank[:, t, :], lhsT=kq_turned[h, g][:, t, :],
                                  rhs=kq_turned[h, i][:, PACK + c, :], start=True, stop=True)
-            banks[n, slot] = bank
+            return bank
 
-        def scale_first(n):
-            table, number = mask_of(*quads[n][0])
-            scaled[n] = stage.tile([P, P, PACK], F32, name="scaled")
-            nc.scalar.activation(out=scaled[n][:], in_=banks[n, 0][:].rearrange("p t n -> p n t"),
-                                 func=ACT.Copy, scale=number)
+        def direct_scores(position):
+            n, r = divmod(position, DIRECT)
+            if live(n):
+                banks[n, r] = keys_on_partitions(psum_vector, "for_vector", *units[n][direct_slot(n, r)])
 
-        def mask_first(n):
-            table, number = mask_of(*quads[n][0])
-            grouped[n] = stage.tile([P, QUAD, P, PACK], BF16, name="grouped", align_bytes=64)
-            nc.gpsimd.tensor_tensor(out=grouped[n][:, 0], in0=scaled[n][:], in1=table, op=ALU.mult)
+        def direct_step(n, r):
+            if live(n):
+                slot = direct_slot(n, r)
+                table, number = table_and_number(*units[n][slot])
+                nc.vector.scalar_tensor_tensor(out=grouped[n][:, slot], in0=banks[n, r][:].rearrange("p t n -> p n t"),
+                                               scalar=number, in1=table, op0=ALU.mult, op1=ALU.mult)
+                direct_scores(DIRECT * n + r + DIRECT_BANKS)
 
-        def mask_rest(n, slot):
-            table, number = mask_of(*quads[n][slot])
-            nc.vector.scalar_tensor_tensor(out=grouped[n][:, slot], in0=banks[n, slot][:].rearrange("p t n -> p n t"),
-                                           scalar=number, in1=table, op0=ALU.mult, op1=ALU.mult)
+        def helped_scores(n, r):
+            if live(n):
+                slot = helped_slot(n, r)
+                table, number = table_and_number(*units[n][slot])
+                bank = keys_on_partitions(psum_scalar, "for_scalar", *units[n][slot])
+                scaled[n, r] = stage.tile([P, P, PACK], F32, name="scaled", bufs=2 * HELPED)
+                nc.scalar.activation(out=scaled[n, r][:], in_=bank[:].rearrange("p t n -> p n t"),
+                                     func=ACT.Copy, scale=number)
+
+        def helped_mask(n, r):
+            if live(n):
+                slot = helped_slot(n, r)
+                table, number = table_and_number(*units[n][slot])
+                nc.gpsimd.tensor_tensor(out=grouped[n][:, slot], in0=scaled[n, r][:], in1=table, op=ALU.mult)
+
+        def detour_out(n):
+            if live(n):
+                h, i, c, g = units[n][detour_slot(n)]
+                wide[n] = psum_scalar.tile([P, PACK, P], F32, name="wide", tag="for_scalar")
+                nc.tensor.matmul(out=wide[n][:].rearrange("n t p -> n (t p)"), lhsT=kq_turned[h, i][:, PACK + c, :],
+                                 rhs=kq_turned[h, g][:, 0:PACK, :].rearrange("d t p -> d (t p)"), start=True, stop=True)
+                rows[n] = stage.tile([P, PACK, P], F32, name="rows")
+                for t in range(PACK):
+                    nc.scalar.activation(out=rows[n][:, t, :], in_=wide[n][:, t, :], func=ACT.Copy,
+                                         scale=row_fac[h][:, t : t + 1])
+
+        def detour_back(n):
+            if live(n):
+                slot = detour_slot(n)
+                h, i, c, g = units[n][slot]
+                j = far_index(i, c, g)
+                back[n] = psum_scalar.tile([P, PACK, P], F32, name="back", tag="for_scalar")
+                for t in range(PACK):
+                    nc.tensor.transpose(back[n][:, t, :], rows[n][:, t, :], identity_f32[:])
+                nc.scalar.activation(out=grouped[n][:, slot], in_=back[n][:].rearrange("p t n -> p n t"),
+                                     func=ACT.Copy, scale=col_fac[h][:, j : j + 1])
 
         def quantise_scores(n):
-            codes[n] = packed.tile([P, QUAD * P], U32, name="codes", align_bytes=64)
-            scales[n] = packed.tile([P, QUAD * P], U8, name="scales", align_bytes=64)
-            nc.vector.quantize_mx(out=codes[n][:].bitcast(FP8X4), scales=scales[n][:],
-                                  in_=grouped[n][:].rearrange("p s n t -> p (s n t)"))
+            if live(n):
+                codes[n] = packed.tile([P, UNIT * P], U32, name="codes", align_bytes=64)
+                scales[n] = packed.tile([P, UNIT * P], U8, name="scales", align_bytes=64)
+                nc.vector.quantize_mx(out=codes[n][:].bitcast(FP8X4), scales=scales[n][:],
+                                      in_=grouped[n][:].rearrange("p s n t -> p (s n t)"))
 
         def attend(n):
-            for slot in range(QUAD):
-                h, i, c, g = quads[n][slot]
-                if c == 0 and g == 0:
-                    sums[h, i] = psum_out.tile([P, TILES, P], F32, name="sums")
-                cols = slice(slot * P, (slot + 1) * P)
-                nc.tensor.matmul_mx(out=sums[h, i][:, c, :],
-                                    lhsT=codes[n][:, cols].bitcast(FP8X4), lhsT_scale=scales[n][:, cols],
-                                    rhs=v_codes[h, g][:].bitcast(FP8X4), rhs_scale=v_scales[h, g][:],
-                                    start=(g == 0), stop=(g == i))
-                if c == TILES - 1 and g == i:
-                    result = results.tile([P, TILES, P], F32)
-                    nc.scalar.copy(out=result[:], in_=sums[h, i][:])
-                    rows = slice(i * GROUP, (i + 1) * GROUP)
-                    nc.sync.dma_start(out=out[0, h, rows, :].rearrange("(c p) d -> p c d", p=P), in_=result[:])
+            if live(n):
+                for slot in range(UNIT):
+                    h, i, c, g = units[n][slot]
+                    if c == 0 and g == 0:
+                        sums[h, i] = psum_out.tile([P, TILES, P], F32, name="sums")
+                    cols = slice(slot * P, (slot + 1) * P)
+                    nc.tensor.matmul_mx(out=sums[h, i][:, c, :],
+                                        lhsT=codes[n][:, cols].bitcast(FP8X4), lhsT_scale=scales[n][:, cols],
+                                        rhs=v_codes[h, g][:].bitcast(FP8X4), rhs_scale=v_scales[h, g][:],
+                                        start=(g == 0), stop=(g == i))
+                    if c == TILES - 1 and g == i:
+                        result = results.tile([P, TILES, P], F32)
+                        nc.scalar.copy(out=result[:], in_=sums[h, i][:])
+                        rows_of_chunk = slice(i * GROUP, (i + 1) * GROUP)
+                        nc.sync.dma_start(out=out[0, h, rows_of_chunk, :].rearrange("(c p) d -> p c d", p=P), in_=result[:])
 
-        last = len(quads)
-        turned_last = (0, 0)
-        for n in range(-2, last + 2):
-            if 0 <= n - 2:
-                attend(n - 2)
-            if 0 <= n < last:
-                mask_rest(n, 1)
-            if 0 <= n - 1 < last:
-                quantise_scores(n - 1)
-            if 0 <= n + 1 < last:
-                mask_first(n + 1)
-            if 0 <= n < last:
-                mask_rest(n, 2)
-                mask_rest(n, 3)
-            if n + 2 < last:
-                scores(n + 2, 0)
-                scale_first(n + 2)
-            if 0 <= n + 1 < last:
-                for slot in range(1, QUAD):
-                    scores(n + 1, slot)
-            if turned_last is not None:
-                quantise_values(*turned_last)
-                turned_last = None
-            if n + 3 < last:
-                h, i, c, g = quads[n + 3][0]
-                if c == 0 and g == 0:
-                    turn_chunk(h, i)
-                    turned_last = (h, i)
-                    s = i - (CHUNKS - NEAR)
-                    if h + 1 < HEADS and s >= 0:
-                        near_table(h + 1, s)
+        def chunks_opening_in(n):
+            return [(h, i) for h, i, c, g in units[n] if c == 0 and g == 0] if live(n) else []
+
+        def next_head_tables(h, i):
+            s = i - (CHUNKS - NEAR)
+            if h + 1 < HEADS and s >= 0:
+                if s == 0:
+                    small_factors(h + 1)
+                near_table(h + 1, s)
+
+        for h, i in chunks_opening_in(0):
+            turn_chunk(h, i)
+        for position in range(DIRECT_BANKS):
+            direct_scores(position)
+        small_factors(0)
+        for s in range(NEAR):
+            near_table(0, s)
+        for n in range(-1, last + 2):
+            detour_out(n + 1)
+            helped_scores(n + 1, 0)
+            direct_step(n, 0)
+            helped_scores(n + 1, 1)
+            direct_step(n, 1)
+
+            quantise_scores(n - 1)
+            if live(n + 1):
+                grouped[n + 1] = stage.tile([P, UNIT, P, PACK], BF16, name="grouped", align_bytes=64)
+            helped_mask(n + 1, 0)
+            helped_mask(n + 1, 1)
+            attend(n - 2)
+            detour_back(n + 1)
+            for h, i in chunks_opening_in(n - 1):
+                quantise_values(h, i)
+            for h, i in chunks_opening_in(n):
+                regroup_values(h, i)
+            for h, i in chunks_opening_in(n + 2):
+                turn_chunk(h, i)
+                next_head_tables(h, i)
+
+            direct_step(n, 2)
+            direct_step(n, 3)
+            direct_step(n, 4)

@@ -19,12 +19,14 @@ CHUNKS = 8
 TILES = 4
 UNIT = 8
 HELPED = 2
-DIRECT = UNIT - HELPED - 1
+DETOURS = (1,)
 DIRECT_BANKS = 3
 NEAR = TILES + 1
 FAR = TILES * (CHUNKS - 1)
 LN_TERMS = 8
 SHIFT = 30.0
+BEYOND = 2.0 ** 115
+LN_MAX = -1e-30
 
 FLOPS = 2 * 2 * P * HEADS * GROUP * GROUP * (CHUNKS * (CHUNKS + 1) // 2)
 
@@ -65,8 +67,7 @@ def tile_multiscaleretention_pa_t_kernel(tc, q, k, v, gamma, out):
                            allow_small_or_imprecise_dtypes=True)
             return numbers
 
-        offsets = count("offsets", [P, PACK], [[1, P], [-1, PACK]], 0, 0)
-        near_steps = count("near_steps", [NEAR], [[P, NEAR]], 0, -PACK)
+        distance = count("distance", [NEAR, P, PACK], [[P, NEAR], [1, P], [-1, PACK]], 0, -PACK)
         far_steps = count("far_steps", [FAR], [[P, FAR]], 0, 0)
         row_steps = count("row_steps", [PACK], [[-1, PACK]], PACK - 1, 1)
         col_steps = count("col_steps", [1], [[0, 1]], GROUP - PACK + 1, -PACK)
@@ -76,6 +77,9 @@ def tile_multiscaleretention_pa_t_kernel(tc, q, k, v, gamma, out):
         shift_down = consts.tile([P, 1], F32)
         nc.vector.memset(shift_up[:], SHIFT)
         nc.vector.memset(shift_down[:], -SHIFT)
+        for s in range(TILES):
+            nc.vector.scalar_tensor_tensor(out=distance[:, s], in0=distance[:, s], scalar=-BEYOND, in1=distance[:, s],
+                                           op0=ALU.mult, op1=ALU.max)
         warm = consts.tile([P, 1], F32)
         nc.scalar.activation(out=warm[:], in_=shift_down[:], func=ACT.Exp)
 
@@ -119,20 +123,16 @@ def tile_multiscaleretention_pa_t_kernel(tc, q, k, v, gamma, out):
                                        op0=ALU.mult, op1=ALU.add)
         nc.vector.scalar_tensor_tensor(out=ln_gamma[:], in0=head_terms[:], scalar=-1.0, in1=tail[:],
                                        op0=ALU.mult, op1=ALU.subtract)
+        nc.vector.tensor_scalar(out=ln_gamma[:], in0=ln_gamma[:], scalar1=LN_MAX, scalar2=None, op0=ALU.min)
 
-        near_bias, col_bias, near, far, row_fac, col_fac = {}, {}, {}, {}, {}, {}
+        col_bias, near, far, row_fac, col_fac = {}, {}, {}, {}, {}
         for h in range(HEADS):
             ln_h = ln_gamma[:, h : h + 1]
-            near_bias[h] = consts.tile([P, NEAR], F32, name="near_bias_%d" % h)
             col_bias[h] = consts.tile([P, 1], F32, name="col_bias_%d" % h)
             near[h] = consts.tile([P, NEAR, P, PACK], F32, name="near_%d" % h)
             far[h] = consts.tile([P, FAR], F32, name="far_%d" % h)
             row_fac[h] = consts.tile([P, PACK], F32, name="row_fac_%d" % h)
             col_fac[h] = consts.tile([P, FAR], F32, name="col_fac_%d" % h)
-            nc.vector.tensor_scalar(out=near_bias[h][:, 0:TILES], in0=near_steps[:, 0:TILES], scalar1=ln_h,
-                                    scalar2=None, op0=ALU.mult)
-            nc.vector.tensor_scalar(out=near_bias[h][:, TILES:NEAR], in0=near_steps[:, TILES:NEAR], scalar1=ln_h,
-                                    scalar2=-SHIFT, op0=ALU.mult, op1=ALU.add)
             nc.vector.tensor_scalar(out=col_bias[h][:], in0=col_steps[:], scalar1=ln_h,
                                     scalar2=SHIFT, op0=ALU.mult, op1=ALU.add)
 
@@ -143,11 +143,11 @@ def tile_multiscaleretention_pa_t_kernel(tc, q, k, v, gamma, out):
             nc.scalar.activation(out=col_fac[h][:], in_=far_steps[:], func=ACT.Exp, scale=ln_h, bias=col_bias[h][:])
 
         def near_table(h, s):
-            nc.scalar.activation(out=near[h][:, s], in_=offsets[:], func=ACT.Exp,
-                                 scale=ln_gamma[:, h : h + 1], bias=near_bias[h][:, s : s + 1])
             if s < TILES:
-                nc.gpsimd.affine_select(out=near[h][:, s], in_=near[h][:, s], pattern=[[1, P], [-1, PACK]],
-                                        compare_op=ALU.is_ge, fill=0.0, base=P * s, channel_multiplier=-PACK)
+                nc.scalar.activation(out=near[h][:, s], in_=distance[:, s], func=ACT.Exp, scale=ln_gamma[:, h : h + 1])
+            else:
+                nc.scalar.activation(out=near[h][:, s], in_=distance[:, s], func=ACT.Exp, scale=ln_gamma[:, h : h + 1],
+                                     bias=shift_down[:])
 
         def far_index(i, c, g):
             return TILES * (i - g - 1) + c
@@ -165,17 +165,23 @@ def tile_multiscaleretention_pa_t_kernel(tc, q, k, v, gamma, out):
         def live(n):
             return 0 <= n < last
 
-        def detour_slot(n):
-            return [slot for slot in range(UNIT) if units[n][slot][3] < units[n][slot][1]][0]
+        def detours(n):
+            return DETOURS[n % len(DETOURS)]
+
+        def detour_slot(n, r):
+            return [slot for slot in range(UNIT) if units[n][slot][3] < units[n][slot][1]][r]
 
         def other_slots(n):
-            return [slot for slot in range(UNIT) if slot != detour_slot(n)]
+            taken = [detour_slot(n, r) for r in range(detours(n))]
+            return [slot for slot in range(UNIT) if slot not in taken]
 
-        def direct_slot(n, r):
-            return other_slots(n)[r]
+        def direct_slots(n):
+            return other_slots(n)[: UNIT - HELPED - detours(n)]
 
         def helped_slot(n, r):
-            return other_slots(n)[DIRECT + r]
+            return other_slots(n)[UNIT - HELPED - detours(n) + r]
+
+        direct_items = [(n, slot) for n in range(last) for slot in direct_slots(n)]
 
         banks, scaled, wide, rows, back, grouped, codes, scales, sums = {}, {}, {}, {}, {}, {}, {}, {}, {}
 
@@ -187,17 +193,17 @@ def tile_multiscaleretention_pa_t_kernel(tc, q, k, v, gamma, out):
             return bank
 
         def direct_scores(position):
-            n, r = divmod(position, DIRECT)
-            if live(n):
-                banks[n, r] = keys_on_partitions(psum_vector, "for_vector", *units[n][direct_slot(n, r)])
+            if position < len(direct_items):
+                n, slot = direct_items[position]
+                banks[n, slot] = keys_on_partitions(psum_vector, "for_vector", *units[n][slot])
 
         def direct_step(n, r):
-            if live(n):
-                slot = direct_slot(n, r)
+            if live(n) and r < len(direct_slots(n)):
+                slot = direct_slots(n)[r]
                 table, number = table_and_number(*units[n][slot])
-                nc.vector.scalar_tensor_tensor(out=grouped[n][:, slot], in0=banks[n, r][:].rearrange("p t n -> p n t"),
+                nc.vector.scalar_tensor_tensor(out=grouped[n][:, slot], in0=banks[n, slot][:].rearrange("p t n -> p n t"),
                                                scalar=number, in1=table, op0=ALU.mult, op1=ALU.mult)
-                direct_scores(DIRECT * n + r + DIRECT_BANKS)
+                direct_scores(direct_items.index((n, slot)) + DIRECT_BANKS)
 
         def helped_scores(n, r):
             if live(n):
@@ -214,26 +220,26 @@ def tile_multiscaleretention_pa_t_kernel(tc, q, k, v, gamma, out):
                 table, number = table_and_number(*units[n][slot])
                 nc.gpsimd.tensor_tensor(out=grouped[n][:, slot], in0=scaled[n, r][:], in1=table, op=ALU.mult)
 
-        def detour_out(n):
-            if live(n):
-                h, i, c, g = units[n][detour_slot(n)]
-                wide[n] = psum_scalar.tile([P, PACK, P], F32, name="wide", tag="for_scalar")
-                nc.tensor.matmul(out=wide[n][:].rearrange("n t p -> n (t p)"), lhsT=kq_turned[h, i][:, PACK + c, :],
+        def detour_out(n, r):
+            if live(n) and r < detours(n):
+                h, i, c, g = units[n][detour_slot(n, r)]
+                wide[n, r] = psum_scalar.tile([P, PACK, P], F32, name="wide", tag="for_scalar")
+                nc.tensor.matmul(out=wide[n, r][:].rearrange("n t p -> n (t p)"), lhsT=kq_turned[h, i][:, PACK + c, :],
                                  rhs=kq_turned[h, g][:, 0:PACK, :].rearrange("d t p -> d (t p)"), start=True, stop=True)
-                rows[n] = stage.tile([P, PACK, P], F32, name="rows")
+                rows[n, r] = stage.tile([P, PACK, P], F32, name="rows", bufs=3)
                 for t in range(PACK):
-                    nc.scalar.activation(out=rows[n][:, t, :], in_=wide[n][:, t, :], func=ACT.Copy,
+                    nc.scalar.activation(out=rows[n, r][:, t, :], in_=wide[n, r][:, t, :], func=ACT.Copy,
                                          scale=row_fac[h][:, t : t + 1])
 
-        def detour_back(n):
-            if live(n):
-                slot = detour_slot(n)
+        def detour_back(n, r):
+            if live(n) and r < detours(n):
+                slot = detour_slot(n, r)
                 h, i, c, g = units[n][slot]
                 j = far_index(i, c, g)
-                back[n] = psum_scalar.tile([P, PACK, P], F32, name="back", tag="for_scalar")
+                back[n, r] = psum_scalar.tile([P, PACK, P], F32, name="back", tag="for_scalar")
                 for t in range(PACK):
-                    nc.tensor.transpose(back[n][:, t, :], rows[n][:, t, :], identity_f32[:])
-                nc.scalar.activation(out=grouped[n][:, slot], in_=back[n][:].rearrange("p t n -> p n t"),
+                    nc.tensor.transpose(back[n, r][:, t, :], rows[n, r][:, t, :], identity_f32[:])
+                nc.scalar.activation(out=grouped[n][:, slot], in_=back[n, r][:].rearrange("p t n -> p n t"),
                                      func=ACT.Copy, scale=col_fac[h][:, j : j + 1])
 
         def quantise_scores(n):
@@ -260,45 +266,50 @@ def tile_multiscaleretention_pa_t_kernel(tc, q, k, v, gamma, out):
                         rows_of_chunk = slice(i * GROUP, (i + 1) * GROUP)
                         nc.sync.dma_start(out=out[0, h, rows_of_chunk, :].rearrange("(c p) d -> p c d", p=P), in_=result[:])
 
-        def chunks_opening_in(n):
-            return [(h, i) for h, i, c, g in units[n] if c == 0 and g == 0] if live(n) else []
+        chunks = [(h, i) for h in range(HEADS) for i in range(CHUNKS)]
 
-        def next_head_tables(h, i):
-            s = i - (CHUNKS - NEAR)
-            if h + 1 < HEADS and s >= 0:
-                if s == 0:
-                    small_factors(h + 1)
-                near_table(h + 1, s)
+        def prepare(n):
+            for j, (h, i) in enumerate(chunks):
+                if j >= 2 and n == 2 * j - 6:
+                    turn_chunk(h, i)
+                if n == max(2 * j - 6, j - 1, 0):
+                    regroup_values(h, i)
+            if n == 5:
+                small_factors(1)
+            if n >= 5 and n % 2 == 1 and (n - 5) // 2 < NEAR:
+                near_table(1, (n - 5) // 2)
 
-        for h, i in chunks_opening_in(0):
-            turn_chunk(h, i)
+        def quantise_prepared(n):
+            for j, (h, i) in enumerate(chunks):
+                if n == max(2 * j - 6, j - 1, 0) + 1:
+                    quantise_values(h, i)
+
+        turn_chunk(0, 0)
+        near_table(0, 0)
+        turn_chunk(0, 1)
         for position in range(DIRECT_BANKS):
             direct_scores(position)
-        small_factors(0)
-        for s in range(NEAR):
+        for s in range(1, NEAR):
             near_table(0, s)
-        for n in range(-1, last + 2):
-            detour_out(n + 1)
-            helped_scores(n + 1, 0)
+        small_factors(0)
+        for n in range(-2, last + 2):
+            detour_out(n + 1, 0)
+            helped_scores(n + 2, 0)
             direct_step(n, 0)
-            helped_scores(n + 1, 1)
+            detour_out(n + 1, 1)
+            helped_scores(n + 2, 1)
             direct_step(n, 1)
 
             quantise_scores(n - 1)
+            quantise_prepared(n)
             if live(n + 1):
                 grouped[n + 1] = stage.tile([P, UNIT, P, PACK], BF16, name="grouped", align_bytes=64)
             helped_mask(n + 1, 0)
             helped_mask(n + 1, 1)
             attend(n - 2)
-            detour_back(n + 1)
-            for h, i in chunks_opening_in(n - 1):
-                quantise_values(h, i)
-            for h, i in chunks_opening_in(n):
-                regroup_values(h, i)
-            for h, i in chunks_opening_in(n + 2):
-                turn_chunk(h, i)
-                next_head_tables(h, i)
-
+            detour_back(n + 1, 0)
             direct_step(n, 2)
+            detour_back(n + 1, 1)
             direct_step(n, 3)
+            prepare(n)
             direct_step(n, 4)

@@ -24,6 +24,7 @@ DIRECT_BANKS = 3
 NEAR = TILES + 1
 FAR = TILES * (CHUNKS - 1)
 LN_TERMS = 8
+CHUNK_ORDER = (1, 0, 2, 3, 4, 5, 6, 7)
 SHIFT = 30.0
 BEYOND = 2.0 ** 115
 LN_MAX = -1e-30
@@ -48,15 +49,29 @@ def tile_multiscaleretention_pa_t_kernel(tc, q, k, v, gamma, out):
         gamma_bf = consts.tile([P, HEADS], BF16)
         nc.sync.dma_start(out=gamma_bf[:], in_=gamma.partition_broadcast(P))
         k_raw, q_raw, v_raw = {}, {}, {}
-        for h in range(HEADS):
-            for i in range(CHUNKS):
-                rows_of_chunk = slice(i * GROUP, (i + 1) * GROUP)
-                k_raw[h, i] = raw.tile([P, PACK, P], BF16, name="k_raw_%d_%d" % (h, i))
-                q_raw[h, i] = raw.tile([P, TILES, P], BF16, name="q_raw_%d_%d" % (h, i))
-                v_raw[h, i] = raw.tile([P, PACK, P], BF16, name="v_raw_%d_%d" % (h, i))
-                nc.sync.dma_start(out=k_raw[h, i][:], in_=k[0, h, rows_of_chunk, :].rearrange("(p t) d -> p t d", t=PACK))
-                nc.sync.dma_start(out=q_raw[h, i][:], in_=q[0, h, rows_of_chunk, :].rearrange("(c p) d -> p c d", p=P))
-                nc.sync.dma_start(out=v_raw[h, i][:], in_=v[0, h, rows_of_chunk, :].rearrange("(p t) d -> p t d", t=PACK))
+        order = [(h, i) for h in range(HEADS) for i in CHUNK_ORDER]
+        turns = [(h, g, i) for (h, i), (same, g) in zip(order, [(h, g) for h in range(HEADS) for g in range(CHUNKS)])]
+        for j, (h, g, i) in enumerate(turns):
+            k_raw[h, g] = raw.tile([P, PACK, P], BF16, name="k_raw_%d_%d" % (h, g))
+            q_raw[h, i] = raw.tile([P, TILES, P], BF16, name="q_raw_%d_%d" % (h, i))
+            v_raw[h, g] = raw.tile([P, PACK, P], BF16, name="v_raw_%d_%d" % (h, g))
+
+        def load_keys_and_queries(j):
+            h, g, i = turns[j]
+            nc.sync.dma_start(out=k_raw[h, g][:], in_=k[0, h, g * GROUP : (g + 1) * GROUP, :].rearrange("(p t) d -> p t d", t=PACK))
+            nc.sync.dma_start(out=q_raw[h, i][:], in_=q[0, h, i * GROUP : (i + 1) * GROUP, :].rearrange("(c p) d -> p c d", p=P))
+
+        def load_values(j):
+            h, g, i = turns[j]
+            nc.sync.dma_start(out=v_raw[h, g][:], in_=v[0, h, g * GROUP : (g + 1) * GROUP, :].rearrange("(p t) d -> p t d", t=PACK))
+
+        load_keys_and_queries(0)
+        load_keys_and_queries(1)
+        load_values(0)
+        load_values(1)
+        for j in range(2, len(turns)):
+            load_keys_and_queries(j)
+            load_values(j)
 
         identity = consts.tile([P, P], BF16)
         make_identity(nc, identity[:])
@@ -67,7 +82,8 @@ def tile_multiscaleretention_pa_t_kernel(tc, q, k, v, gamma, out):
                            allow_small_or_imprecise_dtypes=True)
             return numbers
 
-        distance = count("distance", [NEAR, P, PACK], [[P, NEAR], [1, P], [-1, PACK]], 0, -PACK)
+        offsets = count("offsets", [P, PACK], [[1, P], [-1, PACK]], 0, 0)
+        near_steps = count("near_steps", [NEAR], [[P, NEAR]], 0, -PACK)
         far_steps = count("far_steps", [FAR], [[P, FAR]], 0, 0)
         row_steps = count("row_steps", [PACK], [[-1, PACK]], PACK - 1, 1)
         col_steps = count("col_steps", [1], [[0, 1]], GROUP - PACK + 1, -PACK)
@@ -77,28 +93,36 @@ def tile_multiscaleretention_pa_t_kernel(tc, q, k, v, gamma, out):
         shift_down = consts.tile([P, 1], F32)
         nc.vector.memset(shift_up[:], SHIFT)
         nc.vector.memset(shift_down[:], -SHIFT)
-        for s in range(TILES):
-            nc.vector.scalar_tensor_tensor(out=distance[:, s], in0=distance[:, s], scalar=-BEYOND, in1=distance[:, s],
-                                           op0=ALU.mult, op1=ALU.max)
+
         warm = consts.tile([P, 1], F32)
         nc.scalar.activation(out=warm[:], in_=shift_down[:], func=ACT.Exp)
 
-        kq_turned, v_codes, v_scales, v_grouped = {}, {}, {}, {}
+        causal = consts.tile([P, TILES, P, PACK], F32)
+        for s in range(TILES):
+            nc.gpsimd.affine_select(out=causal[:, s], in_=offsets[:], pattern=[[1, P], [-1, PACK]], compare_op=ALU.is_ge,
+                                    fill=BEYOND, base=P * s, channel_multiplier=-PACK)
 
-        def turn_chunk(h, i):
+        k_turned, q_turned, v_codes, v_scales, v_grouped = {}, {}, {}, {}, {}
+
+        def turn(j):
+            h, g, i = turns[j]
             turned = psum_scalar.tile([P, PACK + TILES, P], BF16, name="turned", tag="for_scalar")
             for t in range(PACK):
-                nc.tensor.transpose(turned[:, t, :], k_raw[h, i][:, t, :], identity[:])
+                nc.tensor.transpose(turned[:, t, :], k_raw[h, g][:, t, :], identity[:])
             for c in range(TILES):
                 nc.tensor.transpose(turned[:, PACK + c, :], q_raw[h, i][:, c, :], identity[:])
-            kq_turned[h, i] = keep.tile([P, PACK + TILES, P], BF16, name="kq_turned_%d_%d" % (h, i))
-            nc.scalar.copy(out=kq_turned[h, i][:], in_=turned[:])
+            kept = keep.tile([P, PACK + TILES, P], BF16, name="kq_turned_%d" % j)
+            nc.scalar.copy(out=kept[:], in_=turned[:])
+            k_turned[h, g] = kept[:, 0:PACK, :]
+            q_turned[h, i] = kept[:, PACK : PACK + TILES, :]
 
-        def regroup_values(h, i):
+        def regroup_values(j):
+            h, i, same = turns[j]
             v_grouped[h, i] = stage.tile([P, P, PACK], BF16, name="v_grouped", align_bytes=64)
             nc.scalar.copy(out=v_grouped[h, i][:], in_=v_raw[h, i][:].rearrange("p t d -> p d t"))
 
-        def quantise_values(h, i):
+        def quantise_values(j):
+            h, i, same = turns[j]
             v_codes[h, i] = keep.tile([P, P], U32, name="v_codes_%d_%d" % (h, i), align_bytes=64)
             v_scales[h, i] = keep.tile([P, P], U8, name="v_scales_%d_%d" % (h, i), align_bytes=64)
             nc.vector.quantize_mx(
@@ -125,14 +149,19 @@ def tile_multiscaleretention_pa_t_kernel(tc, q, k, v, gamma, out):
                                        op0=ALU.mult, op1=ALU.subtract)
         nc.vector.tensor_scalar(out=ln_gamma[:], in0=ln_gamma[:], scalar1=LN_MAX, scalar2=None, op0=ALU.min)
 
-        col_bias, near, far, row_fac, col_fac = {}, {}, {}, {}, {}
+        near_bias, col_bias, near, far, row_fac, col_fac = {}, {}, {}, {}, {}, {}
         for h in range(HEADS):
             ln_h = ln_gamma[:, h : h + 1]
+            near_bias[h] = consts.tile([P, NEAR], F32, name="near_bias_%d" % h)
             col_bias[h] = consts.tile([P, 1], F32, name="col_bias_%d" % h)
             near[h] = consts.tile([P, NEAR, P, PACK], F32, name="near_%d" % h)
             far[h] = consts.tile([P, FAR], F32, name="far_%d" % h)
             row_fac[h] = consts.tile([P, PACK], F32, name="row_fac_%d" % h)
             col_fac[h] = consts.tile([P, FAR], F32, name="col_fac_%d" % h)
+            nc.vector.tensor_scalar(out=near_bias[h][:, TILES:NEAR], in0=near_steps[:, TILES:NEAR], scalar1=ln_h,
+                                    scalar2=-SHIFT, op0=ALU.mult, op1=ALU.add)
+            nc.vector.tensor_scalar(out=near_bias[h][:, 0:TILES], in0=near_steps[:, 0:TILES], scalar1=ln_h,
+                                    scalar2=None, op0=ALU.mult)
             nc.vector.tensor_scalar(out=col_bias[h][:], in0=col_steps[:], scalar1=ln_h,
                                     scalar2=SHIFT, op0=ALU.mult, op1=ALU.add)
 
@@ -143,11 +172,8 @@ def tile_multiscaleretention_pa_t_kernel(tc, q, k, v, gamma, out):
             nc.scalar.activation(out=col_fac[h][:], in_=far_steps[:], func=ACT.Exp, scale=ln_h, bias=col_bias[h][:])
 
         def near_table(h, s):
-            if s < TILES:
-                nc.scalar.activation(out=near[h][:, s], in_=distance[:, s], func=ACT.Exp, scale=ln_gamma[:, h : h + 1])
-            else:
-                nc.scalar.activation(out=near[h][:, s], in_=distance[:, s], func=ACT.Exp, scale=ln_gamma[:, h : h + 1],
-                                     bias=shift_down[:])
+            nc.scalar.activation(out=near[h][:, s], in_=causal[:, s] if s < TILES else offsets[:], func=ACT.Exp,
+                                 scale=ln_gamma[:, h : h + 1], bias=near_bias[h][:, s : s + 1])
 
         def far_index(i, c, g):
             return TILES * (i - g - 1) + c
@@ -158,7 +184,7 @@ def tile_multiscaleretention_pa_t_kernel(tc, q, k, v, gamma, out):
             j = far_index(i, c, g)
             return near[h][:, TILES], far[h][:, j : j + 1]
 
-        items = [(h, i, c, g) for h in range(HEADS) for i in range(CHUNKS) for c in range(TILES) for g in range(i + 1)]
+        items = [(h, i, c, g) for h, i in order for c in range(TILES) for g in range(i + 1)]
         units = [items[a : a + UNIT] for a in range(0, len(items), UNIT)]
         last = len(units)
 
@@ -166,20 +192,22 @@ def tile_multiscaleretention_pa_t_kernel(tc, q, k, v, gamma, out):
             return 0 <= n < last
 
         def detours(n):
-            return DETOURS[n % len(DETOURS)]
+            return 0 if n < 2 else DETOURS[n % len(DETOURS)]
+
+        def helped(n):
+            return 0 if n < 1 else HELPED
+
+        def by_distance(n):
+            return sorted(range(UNIT), key=lambda slot: (units[n][slot][3] == units[n][slot][1], slot))
 
         def detour_slot(n, r):
-            return [slot for slot in range(UNIT) if units[n][slot][3] < units[n][slot][1]][r]
-
-        def other_slots(n):
-            taken = [detour_slot(n, r) for r in range(detours(n))]
-            return [slot for slot in range(UNIT) if slot not in taken]
-
-        def direct_slots(n):
-            return other_slots(n)[: UNIT - HELPED - detours(n)]
+            return by_distance(n)[r]
 
         def helped_slot(n, r):
-            return other_slots(n)[UNIT - HELPED - detours(n) + r]
+            return by_distance(n)[detours(n) + r]
+
+        def direct_slots(n):
+            return by_distance(n)[detours(n) + helped(n) :]
 
         direct_items = [(n, slot) for n in range(last) for slot in direct_slots(n)]
 
@@ -188,8 +216,8 @@ def tile_multiscaleretention_pa_t_kernel(tc, q, k, v, gamma, out):
         def keys_on_partitions(pool, tag, h, i, c, g):
             bank = pool.tile([P, PACK, P], F32, name="bank", tag=tag)
             for t in range(PACK):
-                nc.tensor.matmul(out=bank[:, t, :], lhsT=kq_turned[h, g][:, t, :],
-                                 rhs=kq_turned[h, i][:, PACK + c, :], start=True, stop=True)
+                nc.tensor.matmul(out=bank[:, t, :], lhsT=k_turned[h, g][:, t, :], rhs=q_turned[h, i][:, c, :],
+                                 start=True, stop=True)
             return bank
 
         def direct_scores(position):
@@ -206,7 +234,7 @@ def tile_multiscaleretention_pa_t_kernel(tc, q, k, v, gamma, out):
                 direct_scores(direct_items.index((n, slot)) + DIRECT_BANKS)
 
         def helped_scores(n, r):
-            if live(n):
+            if live(n) and r < helped(n):
                 slot = helped_slot(n, r)
                 table, number = table_and_number(*units[n][slot])
                 bank = keys_on_partitions(psum_scalar, "for_scalar", *units[n][slot])
@@ -215,7 +243,7 @@ def tile_multiscaleretention_pa_t_kernel(tc, q, k, v, gamma, out):
                                      func=ACT.Copy, scale=number)
 
         def helped_mask(n, r):
-            if live(n):
+            if live(n) and r < helped(n):
                 slot = helped_slot(n, r)
                 table, number = table_and_number(*units[n][slot])
                 nc.gpsimd.tensor_tensor(out=grouped[n][:, slot], in0=scaled[n, r][:], in1=table, op=ALU.mult)
@@ -224,8 +252,8 @@ def tile_multiscaleretention_pa_t_kernel(tc, q, k, v, gamma, out):
             if live(n) and r < detours(n):
                 h, i, c, g = units[n][detour_slot(n, r)]
                 wide[n, r] = psum_scalar.tile([P, PACK, P], F32, name="wide", tag="for_scalar")
-                nc.tensor.matmul(out=wide[n, r][:].rearrange("n t p -> n (t p)"), lhsT=kq_turned[h, i][:, PACK + c, :],
-                                 rhs=kq_turned[h, g][:, 0:PACK, :].rearrange("d t p -> d (t p)"), start=True, stop=True)
+                nc.tensor.matmul(out=wide[n, r][:].rearrange("n t p -> n (t p)"), lhsT=q_turned[h, i][:, c, :],
+                                 rhs=k_turned[h, g].rearrange("d t p -> d (t p)"), start=True, stop=True)
                 rows[n, r] = stage.tile([P, PACK, P], F32, name="rows", bufs=3)
                 for t in range(PACK):
                     nc.scalar.activation(out=rows[n, r][:, t, :], in_=wide[n, r][:, t, :], func=ACT.Copy,
@@ -266,50 +294,59 @@ def tile_multiscaleretention_pa_t_kernel(tc, q, k, v, gamma, out):
                         rows_of_chunk = slice(i * GROUP, (i + 1) * GROUP)
                         nc.sync.dma_start(out=out[0, h, rows_of_chunk, :].rearrange("(c p) d -> p c d", p=P), in_=result[:])
 
-        chunks = [(h, i) for h in range(HEADS) for i in range(CHUNKS)]
-
         def prepare(n):
-            for j, (h, i) in enumerate(chunks):
+            for j in range(len(turns)):
                 if j >= 2 and n == 2 * j - 6:
-                    turn_chunk(h, i)
+                    turn(j)
                 if n == max(2 * j - 6, j - 1, 0):
-                    regroup_values(h, i)
+                    regroup_values(j)
             if n == 5:
                 small_factors(1)
             if n >= 5 and n % 2 == 1 and (n - 5) // 2 < NEAR:
                 near_table(1, (n - 5) // 2)
 
         def quantise_prepared(n):
-            for j, (h, i) in enumerate(chunks):
+            for j in range(len(turns)):
                 if n == max(2 * j - 6, j - 1, 0) + 1:
-                    quantise_values(h, i)
+                    quantise_values(j)
 
-        turn_chunk(0, 0)
-        near_table(0, 0)
-        turn_chunk(0, 1)
+        turn(0)
+        turn(1)
+        near_table(0, TILES)
+        small_factors(0)
+        for s in range(TILES):
+            near_table(0, s)
         for position in range(DIRECT_BANKS):
             direct_scores(position)
-        for s in range(1, NEAR):
-            near_table(0, s)
-        small_factors(0)
-        for n in range(-2, last + 2):
-            detour_out(n + 1, 0)
-            helped_scores(n + 2, 0)
+        turn(2)
+        grouped[0] = stage.tile([P, UNIT, P, PACK], BF16, name="grouped", align_bytes=64)
+        direct_step(0, 0)
+        direct_step(0, 1)
+        helped_scores(1, 0)
+        direct_step(0, 2)
+        helped_scores(1, 1)
+        direct_step(0, 3)
+        direct_step(0, 4)
+        direct_step(0, 5)
+        prepare(0)
+        direct_step(0, 6)
+        direct_step(0, 7)
+        for n in range(1, last + 2):
+            if live(n):
+                grouped[n] = stage.tile([P, UNIT, P, PACK], BF16, name="grouped", align_bytes=64)
+            helped_scores(n + 1, 0)
             direct_step(n, 0)
-            detour_out(n + 1, 1)
-            helped_scores(n + 2, 1)
+            helped_scores(n + 1, 1)
             direct_step(n, 1)
-
             quantise_scores(n - 1)
             quantise_prepared(n)
-            if live(n + 1):
-                grouped[n + 1] = stage.tile([P, UNIT, P, PACK], BF16, name="grouped", align_bytes=64)
-            helped_mask(n + 1, 0)
-            helped_mask(n + 1, 1)
+            helped_mask(n, 0)
+            helped_mask(n, 1)
             attend(n - 2)
-            detour_back(n + 1, 0)
+            detour_back(n, 0)
             direct_step(n, 2)
-            detour_back(n + 1, 1)
+            detour_out(n + 1, 0)
             direct_step(n, 3)
             prepare(n)
             direct_step(n, 4)
+            direct_step(n, 5)

@@ -118,7 +118,7 @@ def tile_multiscaleretention_pa_t_kernel(tc, q, k, v, gamma, out):
 
         def regroup_values(j):
             h, i, same = turns[j]
-            v_grouped[h, i] = stage.tile([P, P, PACK], BF16, name="v_grouped", align_bytes=64)
+            v_grouped[h, i] = stage.tile([P, P, PACK], BF16, name="v_grouped", align_bytes=64, bufs=4)
             nc.scalar.copy(out=v_grouped[h, i][:], in_=v_raw[h, i][:].rearrange("p t d -> p d t"))
 
         def quantise_values(j):
@@ -200,14 +200,16 @@ def tile_multiscaleretention_pa_t_kernel(tc, q, k, v, gamma, out):
         def by_distance(n):
             return sorted(range(UNIT), key=lambda slot: (units[n][slot][3] == units[n][slot][1], slot))
 
+        slot_items = [[units[n][a] for a in by_distance(n)] for n in range(last)]
+
         def detour_slot(n, r):
-            return by_distance(n)[r]
+            return r
 
         def helped_slot(n, r):
-            return by_distance(n)[detours(n) + r]
+            return detours(n) + r
 
         def direct_slots(n):
-            return by_distance(n)[detours(n) + helped(n) :]
+            return range(detours(n) + helped(n), UNIT)
 
         direct_items = [(n, slot) for n in range(last) for slot in direct_slots(n)]
 
@@ -223,34 +225,35 @@ def tile_multiscaleretention_pa_t_kernel(tc, q, k, v, gamma, out):
         def direct_scores(position):
             if position < len(direct_items):
                 n, slot = direct_items[position]
-                banks[n, slot] = keys_on_partitions(psum_vector, "for_vector", *units[n][slot])
+                banks[n, slot] = keys_on_partitions(psum_vector, "for_vector", *slot_items[n][slot])
 
         def direct_step(n, r):
             if live(n) and r < len(direct_slots(n)):
                 slot = direct_slots(n)[r]
-                table, number = table_and_number(*units[n][slot])
+                table, number = table_and_number(*slot_items[n][slot])
                 nc.vector.scalar_tensor_tensor(out=grouped[n][:, slot], in0=banks[n, slot][:].rearrange("p t n -> p n t"),
                                                scalar=number, in1=table, op0=ALU.mult, op1=ALU.mult)
                 direct_scores(direct_items.index((n, slot)) + DIRECT_BANKS)
 
         def helped_scores(n, r):
             if live(n) and r < helped(n):
-                slot = helped_slot(n, r)
-                table, number = table_and_number(*units[n][slot])
-                bank = keys_on_partitions(psum_scalar, "for_scalar", *units[n][slot])
-                scaled[n, r] = stage.tile([P, P, PACK], F32, name="scaled", bufs=2 * HELPED)
-                nc.scalar.activation(out=scaled[n, r][:], in_=bank[:].rearrange("p t n -> p n t"),
+                table, number = table_and_number(*slot_items[n][helped_slot(n, r)])
+                bank = keys_on_partitions(psum_scalar, "for_scalar", *slot_items[n][helped_slot(n, r)])
+                if r == 0:
+                    scaled[n] = stage.tile([P, HELPED, P, PACK], F32, name="scaled", bufs=3)
+                nc.scalar.activation(out=scaled[n][:, r], in_=bank[:].rearrange("p t n -> p n t"),
                                      func=ACT.Copy, scale=number)
 
-        def helped_mask(n, r):
-            if live(n) and r < helped(n):
-                slot = helped_slot(n, r)
-                table, number = table_and_number(*units[n][slot])
-                nc.gpsimd.tensor_tensor(out=grouped[n][:, slot], in0=scaled[n, r][:], in1=table, op=ALU.mult)
+        def helped_mask(n):
+            if live(n) and helped(n):
+                slot = helped_slot(n, 0)
+                table, number = table_and_number(*slot_items[n][slot])
+                nc.gpsimd.tensor_tensor(out=grouped[n][:, slot : slot + HELPED], in0=scaled[n][:],
+                                        in1=table.unsqueeze(1).to_broadcast([P, HELPED, P, PACK]), op=ALU.mult)
 
         def detour_out(n, r):
             if live(n) and r < detours(n):
-                h, i, c, g = units[n][detour_slot(n, r)]
+                h, i, c, g = slot_items[n][detour_slot(n, r)]
                 wide[n, r] = psum_scalar.tile([P, PACK, P], F32, name="wide", tag="for_scalar")
                 nc.tensor.matmul(out=wide[n, r][:].rearrange("n t p -> n (t p)"), lhsT=q_turned[h, i][:, c, :],
                                  rhs=k_turned[h, g].rearrange("d t p -> d (t p)"), start=True, stop=True)
@@ -262,7 +265,7 @@ def tile_multiscaleretention_pa_t_kernel(tc, q, k, v, gamma, out):
         def detour_back(n, r):
             if live(n) and r < detours(n):
                 slot = detour_slot(n, r)
-                h, i, c, g = units[n][slot]
+                h, i, c, g = slot_items[n][slot]
                 j = far_index(i, c, g)
                 back[n, r] = psum_scalar.tile([P, PACK, P], F32, name="back", tag="for_scalar")
                 for t in range(PACK):
@@ -279,8 +282,9 @@ def tile_multiscaleretention_pa_t_kernel(tc, q, k, v, gamma, out):
 
         def attend(n):
             if live(n):
-                for slot in range(UNIT):
-                    h, i, c, g = units[n][slot]
+                for item in units[n]:
+                    h, i, c, g = item
+                    slot = slot_items[n].index(item)
                     if c == 0 and g == 0:
                         sums[h, i] = psum_out.tile([P, TILES, P], F32, name="sums")
                     cols = slice(slot * P, (slot + 1) * P)
@@ -294,11 +298,15 @@ def tile_multiscaleretention_pa_t_kernel(tc, q, k, v, gamma, out):
                         rows_of_chunk = slice(i * GROUP, (i + 1) * GROUP)
                         nc.sync.dma_start(out=out[0, h, rows_of_chunk, :].rearrange("(c p) d -> p c d", p=P), in_=result[:])
 
+        def turn_step(j):
+            return 2 * j - 6
+
         def prepare(n):
-            for j in range(len(turns)):
-                if j >= 2 and n == 2 * j - 6:
+            for j in range(3, len(turns)):
+                if n == turn_step(j):
                     turn(j)
-                if n == max(2 * j - 6, j - 1, 0):
+            for j in range(len(turns)):
+                if n == max(turn_step(j), j - 1, 0):
                     regroup_values(j)
             if n == 5:
                 small_factors(1)
@@ -307,45 +315,50 @@ def tile_multiscaleretention_pa_t_kernel(tc, q, k, v, gamma, out):
 
         def quantise_prepared(n):
             for j in range(len(turns)):
-                if n == max(2 * j - 6, j - 1, 0) + 1:
+                if n == max(turn_step(j), j - 1, 0) + 2:
                     quantise_values(j)
 
         turn(0)
         turn(1)
         near_table(0, TILES)
         small_factors(0)
-        for s in range(TILES):
-            near_table(0, s)
+        turn(2)
         for position in range(DIRECT_BANKS):
             direct_scores(position)
-        turn(2)
+        near_table(0, 0)
+        near_table(0, 1)
         grouped[0] = stage.tile([P, UNIT, P, PACK], BF16, name="grouped", align_bytes=64)
         direct_step(0, 0)
         direct_step(0, 1)
         helped_scores(1, 0)
         direct_step(0, 2)
-        helped_scores(1, 1)
         direct_step(0, 3)
+        near_table(0, 2)
+        helped_scores(1, 1)
         direct_step(0, 4)
+        near_table(0, 3)
         direct_step(0, 5)
         prepare(0)
+        helped_scores(2, 0)
+        helped_scores(2, 1)
         direct_step(0, 6)
         direct_step(0, 7)
         for n in range(1, last + 2):
             if live(n):
                 grouped[n] = stage.tile([P, UNIT, P, PACK], BF16, name="grouped", align_bytes=64)
-            helped_scores(n + 1, 0)
+            helped_scores(n + 2, 0)
             direct_step(n, 0)
-            helped_scores(n + 1, 1)
+            helped_scores(n + 2, 1)
             direct_step(n, 1)
-            quantise_scores(n - 1)
             quantise_prepared(n)
-            helped_mask(n, 0)
-            helped_mask(n, 1)
+            quantise_scores(n - 1)
+            helped_mask(n)
             attend(n - 2)
             detour_back(n, 0)
+            detour_back(n, 1)
             direct_step(n, 2)
             detour_out(n + 1, 0)
+            detour_out(n + 1, 1)
             direct_step(n, 3)
             prepare(n)
             direct_step(n, 4)

@@ -23,8 +23,8 @@ DETOURS = (1,)
 DIRECT_BANKS = 3
 NEAR = TILES + 1
 FAR = TILES * (CHUNKS - 1)
-LN_TERMS = 8
 CHUNK_ORDER = (1, 0, 2, 3, 4, 5, 6, 7)
+LN_TERMS = 8
 SHIFT = 30.0
 BEYOND = 2.0 ** 115
 LN_MAX = -1e-30
@@ -131,26 +131,30 @@ def tile_multiscaleretention_pa_t_kernel(tc, q, k, v, gamma, out):
                 in_=v_grouped[h, i][:].rearrange("p d t -> p (d t)"),
             )
 
-        x = consts.tile([P, HEADS], F32)
-        x_sq = consts.tile([P, HEADS], F32)
+        y = consts.tile([P, HEADS], F32)
+        y_sq = consts.tile([P, HEADS], F32)
         tail = consts.tile([P, HEADS], F32)
-        head_terms = consts.tile([P, HEADS], F32)
         ln_gamma = consts.tile([P, HEADS], F32)
-        nc.vector.tensor_scalar(out=x[:], in0=gamma_bf[:], scalar1=-1.0, scalar2=1.0, op0=ALU.mult, op1=ALU.add)
-        nc.vector.tensor_scalar(out=tail[:], in0=x[:], scalar1=1.0 / LN_TERMS, scalar2=None, op0=ALU.mult)
-        for term in range(LN_TERMS - 1, 2, -1):
-            nc.vector.scalar_tensor_tensor(out=tail[:], in0=tail[:], scalar=1.0 / term, in1=x[:],
-                                           op0=ALU.add, op1=ALU.mult)
-        nc.vector.tensor_tensor(out=x_sq[:], in0=x[:], in1=x[:], op=ALU.mult)
-        nc.vector.tensor_tensor(out=tail[:], in0=tail[:], in1=x_sq[:], op=ALU.mult)
-        nc.vector.scalar_tensor_tensor(out=head_terms[:], in0=x_sq[:], scalar=0.5, in1=x[:],
-                                       op0=ALU.mult, op1=ALU.add)
-        nc.vector.scalar_tensor_tensor(out=ln_gamma[:], in0=head_terms[:], scalar=-1.0, in1=tail[:],
-                                       op0=ALU.mult, op1=ALU.subtract)
-        nc.vector.tensor_scalar(out=ln_gamma[:], in0=ln_gamma[:], scalar1=LN_MAX, scalar2=None, op0=ALU.min)
+        heads = [slice(h, h + 1) for h in range(HEADS)]
+        for h in heads:
+            nc.vector.tensor_scalar(out=y[:, h], in0=gamma_bf[:, h], scalar1=1.0, scalar2=-1.0, op0=ALU.mult, op1=ALU.add)
+        for h in heads:
+            nc.vector.tensor_scalar(out=tail[:, h], in0=y[:, h], scalar1=-1.0 / LN_TERMS, scalar2=1.0 / (LN_TERMS - 1),
+                                    op0=ALU.mult, op1=ALU.add)
+        for h in heads:
+            nc.vector.tensor_scalar(out=y_sq[:, h], in0=y[:, h], scalar1=y[:, h], scalar2=None, op0=ALU.mult)
+        for term in range(LN_TERMS - 2, 1, -1):
+            for h in heads:
+                nc.vector.tensor_scalar(out=tail[:, h], in0=tail[:, h], scalar1=y[:, h],
+                                        scalar2=1.0 / term if term % 2 else -1.0 / term, op0=ALU.mult, op1=ALU.add)
+        for h in heads:
+            nc.vector.tensor_scalar(out=ln_gamma[:, h], in0=tail[:, h], scalar1=y_sq[:, h], scalar2=y[:, h],
+                                    op0=ALU.mult, op1=ALU.add)
+        for h in heads:
+            nc.vector.tensor_scalar(out=ln_gamma[:, h], in0=ln_gamma[:, h], scalar1=LN_MAX, scalar2=None, op0=ALU.min)
 
         near_bias, col_bias, near, far, row_fac, col_fac = {}, {}, {}, {}, {}, {}
-        for h in range(HEADS):
+        def biases(h):
             ln_h = ln_gamma[:, h : h + 1]
             near_bias[h] = consts.tile([P, NEAR], F32, name="near_bias_%d" % h)
             col_bias[h] = consts.tile([P, 1], F32, name="col_bias_%d" % h)
@@ -164,6 +168,8 @@ def tile_multiscaleretention_pa_t_kernel(tc, q, k, v, gamma, out):
                                     scalar2=None, op0=ALU.mult)
             nc.vector.tensor_scalar(out=col_bias[h][:], in0=col_steps[:], scalar1=ln_h,
                                     scalar2=SHIFT, op0=ALU.mult, op1=ALU.add)
+
+        biases(0)
 
         def small_factors(h):
             ln_h = ln_gamma[:, h : h + 1]
@@ -192,7 +198,7 @@ def tile_multiscaleretention_pa_t_kernel(tc, q, k, v, gamma, out):
             return 0 <= n < last
 
         def detours(n):
-            return 0 if n < 2 else DETOURS[n % len(DETOURS)]
+            return 0 if n < 2 else 2 if n >= 26 and n % 2 or n % 4 == 1 and n > 8 else 1
 
         def helped(n):
             return 0 if n < 1 else HELPED
@@ -273,12 +279,17 @@ def tile_multiscaleretention_pa_t_kernel(tc, q, k, v, gamma, out):
                 nc.scalar.activation(out=grouped[n][:, slot], in_=back[n, r][:].rearrange("p t n -> p n t"),
                                      func=ACT.Copy, scale=col_fac[h][:, j : j + 1])
 
-        def quantise_scores(n):
+        def quantise_scores(n, begin=0, end=UNIT):
             if live(n):
-                codes[n] = packed.tile([P, UNIT * P], U32, name="codes", align_bytes=64)
-                scales[n] = packed.tile([P, UNIT * P], U8, name="scales", align_bytes=64)
-                nc.vector.quantize_mx(out=codes[n][:].bitcast(FP8X4), scales=scales[n][:],
-                                      in_=grouped[n][:].rearrange("p s n t -> p (s n t)"))
+                if begin == 0:
+                    codes[n] = packed.tile([P, UNIT * P], U32, name="codes", align_bytes=64)
+                    scales[n] = packed.tile([P, UNIT * P], U8, name="scales", align_bytes=64)
+                cols = slice(begin * P, end * P)
+                nc.vector.quantize_mx(out=codes[n][:, cols].bitcast(FP8X4), scales=scales[n][:, cols],
+                                      in_=grouped[n][:, begin:end].rearrange("p s n t -> p (s n t)"))
+
+        store_after = {chunk: {TILES - 1: 0} for chunk in order}
+        store_after[order[-1]] = {TILES - 2: 0, TILES - 1: TILES - 1}
 
         def attend(n):
             if live(n):
@@ -292,11 +303,13 @@ def tile_multiscaleretention_pa_t_kernel(tc, q, k, v, gamma, out):
                                         lhsT=codes[n][:, cols].bitcast(FP8X4), lhsT_scale=scales[n][:, cols],
                                         rhs=v_codes[h, g][:].bitcast(FP8X4), rhs_scale=v_scales[h, g][:],
                                         start=(g == 0), stop=(g == i))
-                    if c == TILES - 1 and g == i:
+                    if g == i and c in store_after[h, i]:
+                        begin = store_after[h, i].get(c)
+                        tiles = slice(begin, c + 1)
                         result = results.tile([P, TILES, P], F32)
-                        nc.scalar.copy(out=result[:], in_=sums[h, i][:])
-                        rows_of_chunk = slice(i * GROUP, (i + 1) * GROUP)
-                        nc.sync.dma_start(out=out[0, h, rows_of_chunk, :].rearrange("(c p) d -> p c d", p=P), in_=result[:])
+                        nc.scalar.copy(out=result[:, tiles], in_=sums[h, i][:, tiles])
+                        rows_of_tiles = slice(i * GROUP + begin * P, i * GROUP + (c + 1) * P)
+                        nc.sync.dma_start(out=out[0, h, rows_of_tiles, :].rearrange("(c p) d -> p c d", p=P), in_=result[:, tiles])
 
         def turn_step(j):
             return 2 * j - 6
@@ -308,6 +321,8 @@ def tile_multiscaleretention_pa_t_kernel(tc, q, k, v, gamma, out):
             for j in range(len(turns)):
                 if n == max(turn_step(j), j - 1, 0):
                     regroup_values(j)
+            if n == 4:
+                biases(1)
             if n == 5:
                 small_factors(1)
             if n >= 5 and n % 2 == 1 and (n - 5) // 2 < NEAR:
@@ -319,9 +334,9 @@ def tile_multiscaleretention_pa_t_kernel(tc, q, k, v, gamma, out):
                     quantise_values(j)
 
         turn(0)
-        turn(1)
         near_table(0, TILES)
         small_factors(0)
+        turn(1)
         turn(2)
         for position in range(DIRECT_BANKS):
             direct_scores(position)
@@ -351,7 +366,8 @@ def tile_multiscaleretention_pa_t_kernel(tc, q, k, v, gamma, out):
             helped_scores(n + 2, 1)
             direct_step(n, 1)
             quantise_prepared(n)
-            quantise_scores(n - 1)
+            if n < last:
+                quantise_scores(n - 1)
             helped_mask(n)
             attend(n - 2)
             detour_back(n, 0)
@@ -360,6 +376,10 @@ def tile_multiscaleretention_pa_t_kernel(tc, q, k, v, gamma, out):
             detour_out(n + 1, 0)
             detour_out(n + 1, 1)
             direct_step(n, 3)
+            if n == last - 1:
+                quantise_scores(n, 0, UNIT // 2)
             prepare(n)
             direct_step(n, 4)
             direct_step(n, 5)
+            if n == last - 1:
+                quantise_scores(n, UNIT // 2, UNIT)

@@ -13,18 +13,19 @@ ACT = mybir.ActivationFunctionType
 
 P = 128
 PACK = 4
+PAIRS = PACK // 2
 GROUP = P * PACK
 HEADS = 2
 CHUNKS = 8
 TILES = 4
 UNIT = 8
 HELPED = 2
-DETOURS = (1,)
 DIRECT_BANKS = 3
-NEAR = TILES + 1
+FLAT = 2
+LIVE = P // TILES
 FAR = TILES * (CHUNKS - 1)
-CHUNK_ORDER = (1, 0, 2, 3, 4, 5, 6, 7)
 LN_TERMS = 8
+CHUNK_ORDER = (3, 2, 1, 0, 4, 5, 6, 7)
 SHIFT = 30.0
 BEYOND = 2.0 ** 115
 LN_MAX = -1e-30
@@ -50,8 +51,8 @@ def tile_multiscaleretention_pa_t_kernel(tc, q, k, v, gamma, out):
         nc.sync.dma_start(out=gamma_bf[:], in_=gamma.partition_broadcast(P))
         k_raw, q_raw, v_raw = {}, {}, {}
         order = [(h, i) for h in range(HEADS) for i in CHUNK_ORDER]
-        turns = [(h, g, i) for (h, i), (same, g) in zip(order, [(h, g) for h in range(HEADS) for g in range(CHUNKS)])]
-        for j, (h, g, i) in enumerate(turns):
+        turns = [(h, a, i) for h in range(HEADS) for a, i in enumerate(CHUNK_ORDER)]
+        for h, g, i in turns:
             k_raw[h, g] = raw.tile([P, PACK, P], BF16, name="k_raw_%d_%d" % (h, g))
             q_raw[h, i] = raw.tile([P, TILES, P], BF16, name="q_raw_%d_%d" % (h, i))
             v_raw[h, g] = raw.tile([P, PACK, P], BF16, name="v_raw_%d_%d" % (h, g))
@@ -65,11 +66,11 @@ def tile_multiscaleretention_pa_t_kernel(tc, q, k, v, gamma, out):
             h, g, i = turns[j]
             nc.sync.dma_start(out=v_raw[h, g][:], in_=v[0, h, g * GROUP : (g + 1) * GROUP, :].rearrange("(p t) d -> p t d", t=PACK))
 
-        load_keys_and_queries(0)
-        load_keys_and_queries(1)
-        load_values(0)
-        load_values(1)
-        for j in range(2, len(turns)):
+        for j in range(4):
+            load_keys_and_queries(j)
+        for j in range(4):
+            load_values(j)
+        for j in range(4, len(turns)):
             load_keys_and_queries(j)
             load_values(j)
 
@@ -83,7 +84,9 @@ def tile_multiscaleretention_pa_t_kernel(tc, q, k, v, gamma, out):
             return numbers
 
         offsets = count("offsets", [P, PACK], [[1, P], [-1, PACK]], 0, 0)
-        near_steps = count("near_steps", [NEAR], [[P, NEAR]], 0, -PACK)
+        key_offsets = count("key_offsets", [FLAT * LIVE, PACK], [[-PACK, FLAT * LIVE], [-1, PACK]], 0, 0)
+        near_steps = count("near_steps", [TILES + 1], [[P, TILES + 1]], 0, -PACK)
+        flat_steps = count("flat_steps", [FLAT], [[P, FLAT]], 0, 1)
         far_steps = count("far_steps", [FAR], [[P, FAR]], 0, 0)
         row_steps = count("row_steps", [PACK], [[-1, PACK]], PACK - 1, 1)
         col_steps = count("col_steps", [1], [[0, 1]], GROUP - PACK + 1, -PACK)
@@ -93,14 +96,24 @@ def tile_multiscaleretention_pa_t_kernel(tc, q, k, v, gamma, out):
         shift_down = consts.tile([P, 1], F32)
         nc.vector.memset(shift_up[:], SHIFT)
         nc.vector.memset(shift_down[:], -SHIFT)
-
         warm = consts.tile([P, 1], F32)
         nc.scalar.activation(out=warm[:], in_=shift_down[:], func=ACT.Exp)
 
-        causal = consts.tile([P, TILES, P, PACK], F32)
-        for s in range(TILES):
-            nc.gpsimd.affine_select(out=causal[:, s], in_=offsets[:], pattern=[[1, P], [-1, PACK]], compare_op=ALU.is_ge,
-                                    fill=BEYOND, base=P * s, channel_multiplier=-PACK)
+        causal = {}
+        for c in range(TILES):
+            flat = c < FLAT
+            width = [(c + 1) * LIVE if flat else P, PACK]
+            causal[c] = consts.tile([P] + width, F32, name="causal_%d" % c)
+            nc.gpsimd.affine_select(out=causal[c][:], in_=key_offsets[:, 0 : (c + 1) * LIVE] if flat else offsets[:],
+                                    pattern=[[-PACK, (c + 1) * LIVE], [-1, PACK]] if flat else [[1, P], [-1, PACK]],
+                                    compare_op=ALU.is_ge, fill=BEYOND, base=P * c, channel_multiplier=1 if flat else -PACK)
+
+        FLAT_BUFS = 3
+        flat_scores = {}
+        for c in range(FLAT):
+            for b in range(FLAT_BUFS):
+                flat_scores[c, b] = consts.tile([P, P, PACK], BF16, name="flat_scores_%d_%d" % (c, b))
+                nc.vector.memset(flat_scores[c, b][:].rearrange("n p t -> n (p t)").bitcast(U32), 0)
 
         k_turned, q_turned, v_codes, v_scales, v_grouped = {}, {}, {}, {}, {}
 
@@ -117,18 +130,18 @@ def tile_multiscaleretention_pa_t_kernel(tc, q, k, v, gamma, out):
             q_turned[h, i] = kept[:, PACK : PACK + TILES, :]
 
         def regroup_values(j):
-            h, i, same = turns[j]
-            v_grouped[h, i] = stage.tile([P, P, PACK], BF16, name="v_grouped", align_bytes=64, bufs=4)
-            nc.scalar.copy(out=v_grouped[h, i][:], in_=v_raw[h, i][:].rearrange("p t d -> p d t"))
+            h, g, i = turns[j]
+            v_grouped[h, g] = stage.tile([P, P, PACK], BF16, name="v_grouped", align_bytes=64, bufs=4)
+            nc.scalar.copy(out=v_grouped[h, g][:], in_=v_raw[h, g][:].rearrange("p t d -> p d t"))
 
         def quantise_values(j):
-            h, i, same = turns[j]
-            v_codes[h, i] = keep.tile([P, P], U32, name="v_codes_%d_%d" % (h, i), align_bytes=64)
-            v_scales[h, i] = keep.tile([P, P], U8, name="v_scales_%d_%d" % (h, i), align_bytes=64)
+            h, g, i = turns[j]
+            v_codes[h, g] = keep.tile([P, P], U32, name="v_codes_%d" % j, align_bytes=64)
+            v_scales[h, g] = keep.tile([P, P], U8, name="v_scales_%d" % j, align_bytes=64)
             nc.vector.quantize_mx(
-                out=v_codes[h, i][:].bitcast(FP8X4),
-                scales=v_scales[h, i][:],
-                in_=v_grouped[h, i][:].rearrange("p d t -> p (d t)"),
+                out=v_codes[h, g][:].bitcast(FP8X4),
+                scales=v_scales[h, g][:],
+                in_=v_grouped[h, g][:].rearrange("p d t -> p (d t)"),
             )
 
         y = consts.tile([P, HEADS], F32)
@@ -153,18 +166,20 @@ def tile_multiscaleretention_pa_t_kernel(tc, q, k, v, gamma, out):
         for h in heads:
             nc.vector.tensor_scalar(out=ln_gamma[:, h], in0=ln_gamma[:, h], scalar1=LN_MAX, scalar2=None, op0=ALU.min)
 
-        near_bias, col_bias, near, far, row_fac, col_fac = {}, {}, {}, {}, {}, {}
+        near_bias, flat_bias, col_bias, near, far, row_fac, col_fac = {}, {}, {}, {}, {}, {}, {}
+
         def biases(h):
             ln_h = ln_gamma[:, h : h + 1]
-            near_bias[h] = consts.tile([P, NEAR], F32, name="near_bias_%d" % h)
+            near_bias[h] = consts.tile([P, TILES + 1], F32, name="near_bias_%d" % h)
+            flat_bias[h] = consts.tile([P, FLAT], F32, name="flat_bias_%d" % h)
             col_bias[h] = consts.tile([P, 1], F32, name="col_bias_%d" % h)
-            near[h] = consts.tile([P, NEAR, P, PACK], F32, name="near_%d" % h)
             far[h] = consts.tile([P, FAR], F32, name="far_%d" % h)
             row_fac[h] = consts.tile([P, PACK], F32, name="row_fac_%d" % h)
             col_fac[h] = consts.tile([P, FAR], F32, name="col_fac_%d" % h)
-            nc.vector.tensor_scalar(out=near_bias[h][:, TILES:NEAR], in0=near_steps[:, TILES:NEAR], scalar1=ln_h,
+            nc.vector.tensor_scalar(out=near_bias[h][:, TILES : TILES + 1], in0=near_steps[:, TILES : TILES + 1], scalar1=ln_h,
                                     scalar2=-SHIFT, op0=ALU.mult, op1=ALU.add)
-            nc.vector.tensor_scalar(out=near_bias[h][:, 0:TILES], in0=near_steps[:, 0:TILES], scalar1=ln_h,
+            nc.vector.tensor_scalar(out=flat_bias[h][:], in0=flat_steps[:], scalar1=ln_h, scalar2=None, op0=ALU.mult)
+            nc.vector.tensor_scalar(out=near_bias[h][:, FLAT:TILES], in0=near_steps[:, FLAT:TILES], scalar1=ln_h,
                                     scalar2=None, op0=ALU.mult)
             nc.vector.tensor_scalar(out=col_bias[h][:], in0=col_steps[:], scalar1=ln_h,
                                     scalar2=SHIFT, op0=ALU.mult, op1=ALU.add)
@@ -178,17 +193,19 @@ def tile_multiscaleretention_pa_t_kernel(tc, q, k, v, gamma, out):
             nc.scalar.activation(out=col_fac[h][:], in_=far_steps[:], func=ACT.Exp, scale=ln_h, bias=col_bias[h][:])
 
         def near_table(h, s):
-            nc.scalar.activation(out=near[h][:, s], in_=causal[:, s] if s < TILES else offsets[:], func=ACT.Exp,
-                                 scale=ln_gamma[:, h : h + 1], bias=near_bias[h][:, s : s + 1])
+            distance = causal[s] if s < TILES else offsets
+            near[h, s] = consts.tile(list(distance.shape), F32, name="near_%d_%d" % (h, s))
+            bias = flat_bias[h][:, s : s + 1] if s < FLAT else near_bias[h][:, s : s + 1]
+            nc.scalar.activation(out=near[h, s][:], in_=distance[:], func=ACT.Exp, scale=ln_gamma[:, h : h + 1], bias=bias)
 
         def far_index(i, c, g):
             return TILES * (i - g - 1) + c
 
         def table_and_number(h, i, c, g):
             if g == i:
-                return near[h][:, c], 1.0
+                return near[h, c][:], 1.0
             j = far_index(i, c, g)
-            return near[h][:, TILES], far[h][:, j : j + 1]
+            return near[h, TILES][:], far[h][:, j : j + 1]
 
         items = [(h, i, c, g) for h, i in order for c in range(TILES) for g in range(i + 1)]
         units = [items[a : a + UNIT] for a in range(0, len(items), UNIT)]
@@ -197,27 +214,39 @@ def tile_multiscaleretention_pa_t_kernel(tc, q, k, v, gamma, out):
         def live(n):
             return 0 <= n < last
 
-        def detours(n):
-            return 0 if n < 2 else 2 if n >= 26 and n % 2 or n % 4 == 1 and n > 8 else 1
+        def is_flat(item):
+            h, i, c, g = item
+            return g == i and c < FLAT
+
+        def below_diagonal(n):
+            return [item for item in units[n] if item[3] < item[1]]
 
         def helped(n):
-            return 0 if n < 1 else HELPED
+            return 0 if n < 1 or len(below_diagonal(n)) < HELPED else HELPED
 
-        def by_distance(n):
-            return sorted(range(UNIT), key=lambda slot: (units[n][slot][3] == units[n][slot][1], slot))
+        def detours(n):
+            f = len([item for item in units[n] if is_flat(item)])
+            w = 0 if n < 3 else 2 if n >= 26 and f == 0 else 1
+            return min(w, len(below_diagonal(n)) - helped(n))
 
-        slot_items = [[units[n][a] for a in by_distance(n)] for n in range(last)]
 
-        def detour_slot(n, r):
-            return r
+        def is_flat(item):
+            h, i, c, g = item
+            return g == i and c < FLAT
 
-        def helped_slot(n, r):
-            return detours(n) + r
+        def arrange(n):
+            below = below_diagonal(n)
+            flat = [item for item in units[n] if is_flat(item)]
+            diagonal = [item for item in units[n] if item[3] == item[1] and not is_flat(item)]
+            taken = detours(n) + helped(n)
+            if n == 0:
+                return sorted(below, key=lambda item: item[3]) + flat + diagonal
+            return below[:taken] + flat + below[taken:] + diagonal
 
-        def direct_slots(n):
-            return range(detours(n) + helped(n), UNIT)
-
-        direct_items = [(n, slot) for n in range(last) for slot in direct_slots(n)]
+        slot_items = [arrange(n) for n in range(last)]
+        direct_items = [(n, slot) for n in range(last) for slot in range(detours(n) + helped(n), UNIT)]
+        first_direct = [direct_items.index((n, detours(n) + helped(n))) for n in range(last)]
+        flat_items = [(n, slot) for n, slot in direct_items if is_flat(slot_items[n][slot])]
 
         banks, scaled, wide, rows, back, grouped, codes, scales, sums = {}, {}, {}, {}, {}, {}, {}, {}, {}
 
@@ -228,23 +257,56 @@ def tile_multiscaleretention_pa_t_kernel(tc, q, k, v, gamma, out):
                                  start=True, stop=True)
             return bank
 
+        def queries_on_partitions(pool, tag, keys, h, i, c, g):
+            bank = pool.tile([P, PACK * P], F32, name="bank", tag=tag)
+            view = bank[:, 0 : PACK * keys].rearrange("n (t p) -> n t p", t=PACK)
+            nc.tensor.matmul(out=view, lhsT=q_turned[h, i][:, c, :], rhs=k_turned[h, g][:, :, 0:keys], start=True, stop=True)
+            return view
+
         def direct_scores(position):
             if position < len(direct_items):
                 n, slot = direct_items[position]
-                banks[n, slot] = keys_on_partitions(psum_vector, "for_vector", *slot_items[n][slot])
+                item = slot_items[n][slot]
+                if is_flat(item):
+                    view = queries_on_partitions(psum_vector, "for_vector", (item[2] + 1) * LIVE, *item)
+                    banks[n, slot] = view.rearrange("n t p -> n p t")
+                else:
+                    bank = keys_on_partitions(psum_vector, "for_vector", *item)
+                    banks[n, slot] = bank[:].rearrange("p t n -> p n t")
+
+        def flat_tile(n, slot):
+            c = slot_items[n][slot][2]
+            turn_number = [pair for pair in flat_items if slot_items[pair[0]][pair[1]][2] == c].index((n, slot))
+            return flat_scores[c, turn_number % FLAT_BUFS]
 
         def direct_step(n, r):
-            if live(n) and r < len(direct_slots(n)):
-                slot = direct_slots(n)[r]
-                table, number = table_and_number(*slot_items[n][slot])
-                nc.vector.scalar_tensor_tensor(out=grouped[n][:, slot], in0=banks[n, slot][:].rearrange("p t n -> p n t"),
-                                               scalar=number, in1=table, op0=ALU.mult, op1=ALU.mult)
-                direct_scores(direct_items.index((n, slot)) + DIRECT_BANKS)
+            if live(n) and detours(n) + helped(n) + r < UNIT:
+                slot = detours(n) + helped(n) + r
+                item = slot_items[n][slot]
+                table, number = table_and_number(*item)
+                if is_flat(item):
+                    target = flat_tile(n, slot)[:, 0 : (item[2] + 1) * LIVE]
+                else:
+                    target = grouped[n][:, slot]
+                nc.vector.scalar_tensor_tensor(out=target, in0=banks[n, slot], scalar=number, in1=table, op0=ALU.mult, op1=ALU.mult)
+                direct_scores(first_direct[n] + r + DIRECT_BANKS)
+
+        def flat_turn(n):
+            if live(n):
+                for slot in range(UNIT):
+                    if is_flat(slot_items[n][slot]):
+                        turned = psum_scalar.tile([P, PAIRS, P], F32, name="flat_turned", tag="for_scalar")
+                        words = flat_tile(n, slot)[:].rearrange("n p t -> n (p t)").bitcast(F32)
+                        for u in range(PAIRS):
+                            nc.tensor.transpose(turned[:, u, :], words[:, u : PAIRS * P : PAIRS], identity_f32[:])
+                        target = grouped[n][:, slot].rearrange("p n t -> p (n t)").bitcast(F32)
+                        nc.scalar.copy(out=target.rearrange("p (n u) -> p n u", u=PAIRS), in_=turned[:].rearrange("p u n -> p n u"))
 
         def helped_scores(n, r):
             if live(n) and r < helped(n):
-                table, number = table_and_number(*slot_items[n][helped_slot(n, r)])
-                bank = keys_on_partitions(psum_scalar, "for_scalar", *slot_items[n][helped_slot(n, r)])
+                slot = detours(n) + r
+                table, number = table_and_number(*slot_items[n][slot])
+                bank = keys_on_partitions(psum_scalar, "for_scalar", *slot_items[n][slot])
                 if r == 0:
                     scaled[n] = stage.tile([P, HELPED, P, PACK], F32, name="scaled", bufs=3)
                 nc.scalar.activation(out=scaled[n][:, r], in_=bank[:].rearrange("p t n -> p n t"),
@@ -252,31 +314,28 @@ def tile_multiscaleretention_pa_t_kernel(tc, q, k, v, gamma, out):
 
         def helped_mask(n):
             if live(n) and helped(n):
-                slot = helped_slot(n, 0)
+                slot = detours(n)
                 table, number = table_and_number(*slot_items[n][slot])
                 nc.gpsimd.tensor_tensor(out=grouped[n][:, slot : slot + HELPED], in0=scaled[n][:],
                                         in1=table.unsqueeze(1).to_broadcast([P, HELPED, P, PACK]), op=ALU.mult)
 
         def detour_out(n, r):
             if live(n) and r < detours(n):
-                h, i, c, g = slot_items[n][detour_slot(n, r)]
-                wide[n, r] = psum_scalar.tile([P, PACK, P], F32, name="wide", tag="for_scalar")
-                nc.tensor.matmul(out=wide[n, r][:].rearrange("n t p -> n (t p)"), lhsT=q_turned[h, i][:, c, :],
-                                 rhs=k_turned[h, g].rearrange("d t p -> d (t p)"), start=True, stop=True)
-                rows[n, r] = stage.tile([P, PACK, P], F32, name="rows", bufs=3)
+                h, i, c, g = slot_items[n][r]
+                wide[n, r] = queries_on_partitions(psum_scalar, "for_scalar", P, h, i, c, g)
+                rows[n, r] = stage.tile([P, PACK, P], F32, name="rows", bufs=6)
                 for t in range(PACK):
                     nc.scalar.activation(out=rows[n, r][:, t, :], in_=wide[n, r][:, t, :], func=ACT.Copy,
                                          scale=row_fac[h][:, t : t + 1])
 
         def detour_back(n, r):
             if live(n) and r < detours(n):
-                slot = detour_slot(n, r)
-                h, i, c, g = slot_items[n][slot]
+                h, i, c, g = slot_items[n][r]
                 j = far_index(i, c, g)
                 back[n, r] = psum_scalar.tile([P, PACK, P], F32, name="back", tag="for_scalar")
                 for t in range(PACK):
                     nc.tensor.transpose(back[n, r][:, t, :], rows[n, r][:, t, :], identity_f32[:])
-                nc.scalar.activation(out=grouped[n][:, slot], in_=back[n, r][:].rearrange("p t n -> p n t"),
+                nc.scalar.activation(out=grouped[n][:, r], in_=back[n, r][:].rearrange("p t n -> p n t"),
                                      func=ACT.Copy, scale=col_fac[h][:, j : j + 1])
 
         def quantise_scores(n, begin=0, end=UNIT):
@@ -314,53 +373,60 @@ def tile_multiscaleretention_pa_t_kernel(tc, q, k, v, gamma, out):
         def turn_step(j):
             return 2 * j - 6
 
+        def regroup_step(j):
+            return max(turn_step(j), j // 2)
+
         def prepare(n):
-            for j in range(3, len(turns)):
-                if n == turn_step(j):
-                    turn(j)
             for j in range(len(turns)):
-                if n == max(turn_step(j), j - 1, 0):
+                if j > 3 and n == turn_step(j):
+                    turn(j)
+                if n == regroup_step(j):
                     regroup_values(j)
             if n == 4:
                 biases(1)
             if n == 5:
                 small_factors(1)
-            if n >= 5 and n % 2 == 1 and (n - 5) // 2 < NEAR:
+            if n >= 5 and n % 2 == 1 and (n - 5) // 2 <= TILES:
                 near_table(1, (n - 5) // 2)
 
         def quantise_prepared(n):
             for j in range(len(turns)):
-                if n == max(turn_step(j), j - 1, 0) + 2:
+                if n == regroup_step(j) + 2:
                     quantise_values(j)
 
         turn(0)
         near_table(0, TILES)
         small_factors(0)
-        turn(1)
-        turn(2)
-        for position in range(DIRECT_BANKS):
+        for position in range(2):
             direct_scores(position)
-        near_table(0, 0)
-        near_table(0, 1)
+        turn(1)
+        direct_scores(2)
+        turn(2)
         grouped[0] = stage.tile([P, UNIT, P, PACK], BF16, name="grouped", align_bytes=64)
         direct_step(0, 0)
         direct_step(0, 1)
-        helped_scores(1, 0)
+        turn(3)
+        for s in range(FLAT):
+            near_table(0, s)
         direct_step(0, 2)
+        helped_scores(1, 0)
         direct_step(0, 3)
-        near_table(0, 2)
         helped_scores(1, 1)
         direct_step(0, 4)
-        near_table(0, 3)
         direct_step(0, 5)
+        near_table(0, 2)
+        near_table(0, 3)
         prepare(0)
+        grouped[1] = stage.tile([P, UNIT, P, PACK], BF16, name="grouped", align_bytes=64)
+        helped_mask(1)
+        detour_out(2, 0)
         helped_scores(2, 0)
         helped_scores(2, 1)
         direct_step(0, 6)
         direct_step(0, 7)
+        flat_turn(0)
+
         for n in range(1, last + 2):
-            if live(n):
-                grouped[n] = stage.tile([P, UNIT, P, PACK], BF16, name="grouped", align_bytes=64)
             helped_scores(n + 2, 0)
             direct_step(n, 0)
             helped_scores(n + 2, 1)
@@ -368,16 +434,25 @@ def tile_multiscaleretention_pa_t_kernel(tc, q, k, v, gamma, out):
             quantise_prepared(n)
             if n < last:
                 quantise_scores(n - 1)
-            helped_mask(n)
-            attend(n - 2)
-            detour_back(n, 0)
-            detour_back(n, 1)
+            if live(n + 1):
+                grouped[n + 1] = stage.tile([P, UNIT, P, PACK], BF16, name="grouped", align_bytes=64)
+            helped_mask(n + 1)
+            detour_out(n + 2, 0)
+            for m in range(last):
+                if n == max(m + 2, 3):
+                    attend(m)
+            flat_turn(n)
             direct_step(n, 2)
-            detour_out(n + 1, 0)
-            detour_out(n + 1, 1)
+            detour_back(n + 1, 0)
+            if live(n + 2):
+                for r in range(1, detours(n + 2)):
+                    detour_out(n + 2, r)
             direct_step(n, 3)
             if n == last - 1:
                 quantise_scores(n, 0, UNIT // 2)
+            if live(n + 1):
+                for r in range(1, detours(n + 1)):
+                    detour_back(n + 1, r)
             prepare(n)
             direct_step(n, 4)
             direct_step(n, 5)

@@ -51,27 +51,35 @@ def tile_multiscaleretention_pa_t_kernel(tc, q, k, v, gamma, out):
         nc.sync.dma_start(out=gamma_bf[:], in_=gamma.partition_broadcast(P))
         k_raw, q_raw, v_raw = {}, {}, {}
         order = [(h, i) for h in range(HEADS) for i in CHUNK_ORDER]
-        turns = [(h, a, i) for h in range(HEADS) for a, i in enumerate(CHUNK_ORDER)]
-        for h, g, i in turns:
+        first_pieces = (("k", 0), ("q", 3), ("k", 1), ("k", 2), ("k", 3), ("q", 2), ("q", 1), ("q", 0))
+        pieces = first_pieces + tuple((kind, i) for i in range(TILES, CHUNKS) for kind in ("k", "q"))
+        turns = [(h, pieces[a], pieces[a + 1]) for h in range(HEADS) for a in range(0, len(pieces), 2)]
+        groups = [(h, g) for h in range(HEADS) for g in range(CHUNKS)]
+        for h, g in groups:
             k_raw[h, g] = raw.tile([P, PACK, P], BF16, name="k_raw_%d_%d" % (h, g))
-            q_raw[h, i] = raw.tile([P, TILES, P], BF16, name="q_raw_%d_%d" % (h, i))
+            q_raw[h, g] = raw.tile([P, TILES, P], BF16, name="q_raw_%d_%d" % (h, g))
             v_raw[h, g] = raw.tile([P, PACK, P], BF16, name="v_raw_%d_%d" % (h, g))
 
-        def load_keys_and_queries(j):
-            h, g, i = turns[j]
-            nc.sync.dma_start(out=k_raw[h, g][:], in_=k[0, h, g * GROUP : (g + 1) * GROUP, :].rearrange("(p t) d -> p t d", t=PACK))
-            nc.sync.dma_start(out=q_raw[h, i][:], in_=q[0, h, i * GROUP : (i + 1) * GROUP, :].rearrange("(c p) d -> p c d", p=P))
+        def load_pieces(j):
+            h = turns[j][0]
+            for kind, i in turns[j][1:]:
+                rows_of_piece = slice(i * GROUP, (i + 1) * GROUP)
+                if kind == "k":
+                    nc.sync.dma_start(out=k_raw[h, i][:], in_=k[0, h, rows_of_piece, :].rearrange("(p t) d -> p t d", t=PACK))
+                else:
+                    nc.sync.dma_start(out=q_raw[h, i][:], in_=q[0, h, rows_of_piece, :].rearrange("(c p) d -> p c d", p=P))
 
         def load_values(j):
-            h, g, i = turns[j]
+            h, g = groups[j]
             nc.sync.dma_start(out=v_raw[h, g][:], in_=v[0, h, g * GROUP : (g + 1) * GROUP, :].rearrange("(p t) d -> p t d", t=PACK))
 
-        for j in range(4):
-            load_keys_and_queries(j)
+        for j in range(3):
+            load_pieces(j)
         for j in range(4):
             load_values(j)
+        load_pieces(3)
         for j in range(4, len(turns)):
-            load_keys_and_queries(j)
+            load_pieces(j)
             load_values(j)
 
         identity = consts.tile([P, P], BF16)
@@ -118,24 +126,27 @@ def tile_multiscaleretention_pa_t_kernel(tc, q, k, v, gamma, out):
         k_turned, q_turned, v_codes, v_scales, v_grouped = {}, {}, {}, {}, {}
 
         def turn(j):
-            h, g, i = turns[j]
-            turned = psum_scalar.tile([P, PACK + TILES, P], BF16, name="turned", tag="for_scalar")
-            for t in range(PACK):
-                nc.tensor.transpose(turned[:, t, :], k_raw[h, g][:, t, :], identity[:])
-            for c in range(TILES):
-                nc.tensor.transpose(turned[:, PACK + c, :], q_raw[h, i][:, c, :], identity[:])
-            kept = keep.tile([P, PACK + TILES, P], BF16, name="kq_turned_%d" % j)
+            h = turns[j][0]
+            turned = psum_scalar.tile([P, 2 * PACK, P], BF16, name="turned", tag="for_scalar")
+            kept = keep.tile([P, 2 * PACK, P], BF16, name="kq_turned_%d" % j)
+            for half, (kind, i) in enumerate(turns[j][1:]):
+                piece = k_raw[h, i] if kind == "k" else q_raw[h, i]
+                planes = slice(half * PACK, (half + 1) * PACK)
+                for a in range(PACK):
+                    nc.tensor.transpose(turned[:, half * PACK + a, :], piece[:, a, :], identity[:])
+                if kind == "k":
+                    k_turned[h, i] = kept[:, planes, :]
+                else:
+                    q_turned[h, i] = kept[:, planes, :]
             nc.scalar.copy(out=kept[:], in_=turned[:])
-            k_turned[h, g] = kept[:, 0:PACK, :]
-            q_turned[h, i] = kept[:, PACK : PACK + TILES, :]
 
         def regroup_values(j):
-            h, g, i = turns[j]
+            h, g = groups[j]
             v_grouped[h, g] = stage.tile([P, P, PACK], BF16, name="v_grouped", align_bytes=64, bufs=4)
             nc.scalar.copy(out=v_grouped[h, g][:], in_=v_raw[h, g][:].rearrange("p t d -> p d t"))
 
         def quantise_values(j):
-            h, g, i = turns[j]
+            h, g = groups[j]
             v_codes[h, g] = keep.tile([P, P], U32, name="v_codes_%d" % j, align_bytes=64)
             v_scales[h, g] = keep.tile([P, P], U8, name="v_scales_%d" % j, align_bytes=64)
             nc.vector.quantize_mx(
@@ -149,11 +160,9 @@ def tile_multiscaleretention_pa_t_kernel(tc, q, k, v, gamma, out):
         tail = consts.tile([P, HEADS], F32)
         ln_gamma = consts.tile([P, HEADS], F32)
         heads = [slice(h, h + 1) for h in range(HEADS)]
-        for h in heads:
-            nc.vector.tensor_scalar(out=y[:, h], in0=gamma_bf[:, h], scalar1=1.0, scalar2=-1.0, op0=ALU.mult, op1=ALU.add)
-        for h in heads:
-            nc.vector.tensor_scalar(out=tail[:, h], in0=y[:, h], scalar1=-1.0 / LN_TERMS, scalar2=1.0 / (LN_TERMS - 1),
-                                    op0=ALU.mult, op1=ALU.add)
+        nc.vector.tensor_scalar(out=y[:], in0=gamma_bf[:], scalar1=-1.0, scalar2=LN_MAX, op0=ALU.add, op1=ALU.min)
+        nc.vector.tensor_scalar(out=tail[:], in0=y[:], scalar1=-1.0 / LN_TERMS, scalar2=1.0 / (LN_TERMS - 1),
+                                op0=ALU.mult, op1=ALU.add)
         for h in heads:
             nc.vector.tensor_scalar(out=y_sq[:, h], in0=y[:, h], scalar1=y[:, h], scalar2=None, op0=ALU.mult)
         for term in range(LN_TERMS - 2, 1, -1):
@@ -163,8 +172,6 @@ def tile_multiscaleretention_pa_t_kernel(tc, q, k, v, gamma, out):
         for h in heads:
             nc.vector.tensor_scalar(out=ln_gamma[:, h], in0=tail[:, h], scalar1=y_sq[:, h], scalar2=y[:, h],
                                     op0=ALU.mult, op1=ALU.add)
-        for h in heads:
-            nc.vector.tensor_scalar(out=ln_gamma[:, h], in0=ln_gamma[:, h], scalar1=LN_MAX, scalar2=None, op0=ALU.min)
 
         near_bias, flat_bias, col_bias, near, far, row_fac, col_fac = {}, {}, {}, {}, {}, {}, {}
 
@@ -186,9 +193,11 @@ def tile_multiscaleretention_pa_t_kernel(tc, q, k, v, gamma, out):
 
         biases(0)
 
-        def small_factors(h):
+        def far_factors(h):
+            nc.scalar.activation(out=far[h][:], in_=far_steps[:], func=ACT.Exp, scale=ln_gamma[:, h : h + 1], bias=shift_up[:])
+
+        def detour_factors(h):
             ln_h = ln_gamma[:, h : h + 1]
-            nc.scalar.activation(out=far[h][:], in_=far_steps[:], func=ACT.Exp, scale=ln_h, bias=shift_up[:])
             nc.scalar.activation(out=row_fac[h][:], in_=row_steps[:], func=ACT.Exp, scale=ln_h, bias=shift_down[:])
             nc.scalar.activation(out=col_fac[h][:], in_=far_steps[:], func=ACT.Exp, scale=ln_h, bias=col_bias[h][:])
 
@@ -226,7 +235,7 @@ def tile_multiscaleretention_pa_t_kernel(tc, q, k, v, gamma, out):
 
         def detours(n):
             f = len([item for item in units[n] if is_flat(item)])
-            w = 0 if n < 3 else 2 if n >= 26 and f == 0 else 1
+            w = 0 if n < 3 else 3 if n == 35 else 2 if n >= 26 and f == 0 or n >= 33 else 1
             return min(w, len(below_diagonal(n)) - helped(n))
 
 
@@ -240,7 +249,8 @@ def tile_multiscaleretention_pa_t_kernel(tc, q, k, v, gamma, out):
             diagonal = [item for item in units[n] if item[3] == item[1] and not is_flat(item)]
             taken = detours(n) + helped(n)
             if n == 0:
-                return sorted(below, key=lambda item: item[3]) + flat + diagonal
+                below = sorted(below, key=lambda item: item[3])
+                return below[:4] + flat + below[4:] + diagonal
             return below[:taken] + flat + below[taken:] + diagonal
 
         slot_items = [arrange(n) for n in range(last)]
@@ -385,7 +395,8 @@ def tile_multiscaleretention_pa_t_kernel(tc, q, k, v, gamma, out):
             if n == 4:
                 biases(1)
             if n == 5:
-                small_factors(1)
+                far_factors(1)
+                detour_factors(1)
             if n >= 5 and n % 2 == 1 and (n - 5) // 2 <= TILES:
                 near_table(1, (n - 5) // 2)
 
@@ -395,17 +406,16 @@ def tile_multiscaleretention_pa_t_kernel(tc, q, k, v, gamma, out):
                     quantise_values(j)
 
         turn(0)
+        far_factors(0)
         near_table(0, TILES)
-        small_factors(0)
-        for position in range(2):
-            direct_scores(position)
+        direct_scores(0)
         turn(1)
+        direct_scores(1)
         direct_scores(2)
-        turn(2)
         grouped[0] = stage.tile([P, UNIT, P, PACK], BF16, name="grouped", align_bytes=64)
+        turn(2)
         direct_step(0, 0)
         direct_step(0, 1)
-        turn(3)
         for s in range(FLAT):
             near_table(0, s)
         direct_step(0, 2)
@@ -414,18 +424,19 @@ def tile_multiscaleretention_pa_t_kernel(tc, q, k, v, gamma, out):
         helped_scores(1, 1)
         direct_step(0, 4)
         direct_step(0, 5)
+        flat_turn(0)
+        turn(3)
         near_table(0, 2)
         near_table(0, 3)
         prepare(0)
         grouped[1] = stage.tile([P, UNIT, P, PACK], BF16, name="grouped", align_bytes=64)
         helped_mask(1)
+        detour_factors(0)
         detour_out(2, 0)
         helped_scores(2, 0)
         helped_scores(2, 1)
         direct_step(0, 6)
         direct_step(0, 7)
-        flat_turn(0)
-
         for n in range(1, last + 2):
             helped_scores(n + 2, 0)
             direct_step(n, 0)

@@ -75,9 +75,11 @@ def tile_multiscaleretention_pa_t_kernel(tc, q, k, v, gamma, out):
 
         for j in range(3):
             load_pieces(j)
-        for j in range(4):
+        for j in range(2):
             load_values(j)
         load_pieces(3)
+        for j in range(2, 4):
+            load_values(j)
         for j in range(4, len(turns)):
             load_pieces(j)
             load_values(j)
@@ -235,7 +237,7 @@ def tile_multiscaleretention_pa_t_kernel(tc, q, k, v, gamma, out):
 
         def detours(n):
             f = len([item for item in units[n] if is_flat(item)])
-            w = 0 if n < 3 else 3 if n == 35 else 2 if n >= 26 and f == 0 or n >= 33 else 1
+            w = 0 if n < 3 else 2 if n >= 26 and f == 0 else 1
             return min(w, len(below_diagonal(n)) - helped(n))
 
 
@@ -425,7 +427,6 @@ def tile_multiscaleretention_pa_t_kernel(tc, q, k, v, gamma, out):
         direct_step(0, 4)
         direct_step(0, 5)
         flat_turn(0)
-        turn(3)
         near_table(0, 2)
         near_table(0, 3)
         prepare(0)
@@ -437,6 +438,7 @@ def tile_multiscaleretention_pa_t_kernel(tc, q, k, v, gamma, out):
         helped_scores(2, 1)
         direct_step(0, 6)
         direct_step(0, 7)
+        turn(3)
         for n in range(1, last + 2):
             helped_scores(n + 2, 0)
             direct_step(n, 0)

@@ -100,8 +100,6 @@ def tile_multiscaleretention_pa_t_kernel(tc, q, k, v, gamma, out):
         far_steps = count("far_steps", [FAR], [[P, FAR]], 0, 0)
         row_steps = count("row_steps", [PACK], [[-1, PACK]], PACK - 1, 1)
         col_steps = count("col_steps", [1], [[0, 1]], GROUP - PACK + 1, -PACK)
-        identity_f32 = consts.tile([P, P], F32)
-        make_identity(nc, identity_f32[:])
         shift_up = consts.tile([P, 1], F32)
         shift_down = consts.tile([P, 1], F32)
         nc.vector.memset(shift_up[:], SHIFT)
@@ -109,8 +107,11 @@ def tile_multiscaleretention_pa_t_kernel(tc, q, k, v, gamma, out):
         warm = consts.tile([P, 1], F32)
         nc.scalar.activation(out=warm[:], in_=shift_down[:], func=ACT.Exp)
 
+        identity_f32 = consts.tile([P, P], F32)
         causal = {}
         for c in range(TILES):
+            if c == FLAT:
+                make_identity(nc, identity_f32[:])
             flat = c < FLAT
             width = [(c + 1) * LIVE if flat else P, PACK]
             causal[c] = consts.tile([P] + width, F32, name="causal_%d" % c)
@@ -118,12 +119,15 @@ def tile_multiscaleretention_pa_t_kernel(tc, q, k, v, gamma, out):
                                     pattern=[[-PACK, (c + 1) * LIVE], [-1, PACK]] if flat else [[1, P], [-1, PACK]],
                                     compare_op=ALU.is_ge, fill=BEYOND, base=P * c, channel_multiplier=1 if flat else -PACK)
 
-        FLAT_BUFS = 3
+
+        FLAT_BUFS = 2
         flat_scores = {}
         for c in range(FLAT):
             for b in range(FLAT_BUFS):
                 flat_scores[c, b] = consts.tile([P, P, PACK], BF16, name="flat_scores_%d_%d" % (c, b))
-                nc.vector.memset(flat_scores[c, b][:].rearrange("n p t -> n (p t)").bitcast(U32), 0)
+                dead = flat_scores[c, b][:, (c + 1) * LIVE : P]
+                nc.scalar.activation(out=dead.rearrange("n p t -> n (p t)"), in_=shift_down[:].to_broadcast([P, (P - (c + 1) * LIVE) * PACK]),
+                                     func=ACT.Copy, scale=0.0)
 
         k_turned, q_turned, v_codes, v_scales, v_grouped = {}, {}, {}, {}, {}
 
@@ -162,9 +166,11 @@ def tile_multiscaleretention_pa_t_kernel(tc, q, k, v, gamma, out):
         tail = consts.tile([P, HEADS], F32)
         ln_gamma = consts.tile([P, HEADS], F32)
         heads = [slice(h, h + 1) for h in range(HEADS)]
-        nc.vector.tensor_scalar(out=y[:], in0=gamma_bf[:], scalar1=-1.0, scalar2=LN_MAX, op0=ALU.add, op1=ALU.min)
-        nc.vector.tensor_scalar(out=tail[:], in0=y[:], scalar1=-1.0 / LN_TERMS, scalar2=1.0 / (LN_TERMS - 1),
-                                op0=ALU.mult, op1=ALU.add)
+        for h in heads:
+            nc.vector.tensor_scalar(out=y[:, h], in0=gamma_bf[:, h], scalar1=-1.0, scalar2=LN_MAX, op0=ALU.add, op1=ALU.min)
+        for h in heads:
+            nc.vector.tensor_scalar(out=tail[:, h], in0=y[:, h], scalar1=-1.0 / LN_TERMS, scalar2=1.0 / (LN_TERMS - 1),
+                                    op0=ALU.mult, op1=ALU.add)
         for h in heads:
             nc.vector.tensor_scalar(out=y_sq[:, h], in0=y[:, h], scalar1=y[:, h], scalar2=None, op0=ALU.mult)
         for term in range(LN_TERMS - 2, 1, -1):
@@ -185,11 +191,14 @@ def tile_multiscaleretention_pa_t_kernel(tc, q, k, v, gamma, out):
             far[h] = consts.tile([P, FAR], F32, name="far_%d" % h)
             row_fac[h] = consts.tile([P, PACK], F32, name="row_fac_%d" % h)
             col_fac[h] = consts.tile([P, FAR], F32, name="col_fac_%d" % h)
-            nc.vector.tensor_scalar(out=near_bias[h][:, TILES : TILES + 1], in0=near_steps[:, TILES : TILES + 1], scalar1=ln_h,
-                                    scalar2=-SHIFT, op0=ALU.mult, op1=ALU.add)
-            nc.vector.tensor_scalar(out=flat_bias[h][:], in0=flat_steps[:], scalar1=ln_h, scalar2=None, op0=ALU.mult)
-            nc.vector.tensor_scalar(out=near_bias[h][:, FLAT:TILES], in0=near_steps[:, FLAT:TILES], scalar1=ln_h,
-                                    scalar2=None, op0=ALU.mult)
+            for s in [TILES] + list(range(TILES)):
+                column = slice(s, s + 1)
+                if s < FLAT:
+                    nc.vector.tensor_scalar(out=flat_bias[h][:, column], in0=flat_steps[:, column], scalar1=ln_h,
+                                            scalar2=None, op0=ALU.mult)
+                else:
+                    nc.vector.tensor_scalar(out=near_bias[h][:, column], in0=near_steps[:, column], scalar1=ln_h,
+                                            scalar2=-SHIFT if s == TILES else 0.0, op0=ALU.mult, op1=ALU.add)
             nc.vector.tensor_scalar(out=col_bias[h][:], in0=col_steps[:], scalar1=ln_h,
                                     scalar2=SHIFT, op0=ALU.mult, op1=ALU.add)
 

@@ -18,6 +18,7 @@ GROUP = P * PACK
 HEADS = 2
 CHUNKS = 8
 TILES = 4
+RUN = 4
 UNIT = 8
 HELPED = 2
 DIRECT_BANKS = 3
@@ -149,7 +150,8 @@ def tile_multiscaleretention_pa_t_kernel(tc, q, k, v, gamma, out):
         def regroup_values(j):
             h, g = groups[j]
             v_grouped[h, g] = stage.tile([P, P, PACK], BF16, name="v_grouped", align_bytes=64, bufs=4)
-            nc.scalar.copy(out=v_grouped[h, g][:], in_=v_raw[h, g][:].rearrange("p t d -> p d t"))
+            nc.scalar.copy(out=v_grouped[h, g][:].rearrange("p (c a) t -> p c t a", a=RUN),
+                           in_=v_raw[h, g][:].rearrange("p t (c a) -> p c t a", a=RUN))
 
         def quantise_values(j):
             h, g = groups[j]
@@ -246,7 +248,7 @@ def tile_multiscaleretention_pa_t_kernel(tc, q, k, v, gamma, out):
 
         def detours(n):
             f = len([item for item in units[n] if is_flat(item)])
-            w = 0 if n < 3 else 2 if n >= 26 and f == 0 else 1
+            w = 0 if n < 3 else 3 if n == 35 else 2 if n >= 26 and f == 0 or n >= 33 else 1
             return min(w, len(below_diagonal(n)) - helped(n))
 
 

from contextlib import ExitStack

import concourse.mybir as mybir
from concourse.masks import make_identity

F32 = mybir.dt.float32
BF16 = mybir.dt.bfloat16
U32 = mybir.dt.uint32
U8 = mybir.dt.uint8
FP8X4 = mybir.dt.float8_e4m3fn_x4
ALU = mybir.AluOpType
ACT = mybir.ActivationFunctionType

P = 128
PACK = 4
PAIRS = PACK // 2
GROUP = P * PACK
HEADS = 2
CHUNKS = 8
TILES = 4
RUN = 4
UNIT = 8
HELPED = 2
DIRECT_BANKS = 3
FLAT = 2
LIVE = P // TILES
FAR = TILES * (CHUNKS - 1)
LN_TERMS = 8
CHUNK_ORDER = (3, 2, 1, 0, 4, 5, 6, 7)
SHIFT = 30.0
BEYOND = 2.0 ** 115
LN_MAX = -1e-30

FLOPS = 2 * 2 * P * HEADS * GROUP * GROUP * (CHUNKS * (CHUNKS + 1) // 2)


def tile_multiscaleretention_pa_t_kernel(tc, q, k, v, gamma, out):
    nc = tc.nc
    with ExitStack() as ctx:
        consts = ctx.enter_context(tc.tile_pool(name="consts", bufs=1))
        raw = ctx.enter_context(tc.tile_pool(name="raw", bufs=1))
        keep = ctx.enter_context(tc.tile_pool(name="keep", bufs=1))
        stage = ctx.enter_context(tc.tile_pool(name="stage", bufs=2))
        packed = ctx.enter_context(tc.tile_pool(name="packed", bufs=3))
        results = ctx.enter_context(tc.tile_pool(name="results", bufs=3))
        psum_vector = ctx.enter_context(tc.psum_pool(name="psum_vector", bufs=DIRECT_BANKS))
        psum_scalar = ctx.enter_context(tc.psum_pool(name="psum_scalar", bufs=3))
        psum_out = ctx.enter_context(tc.psum_pool(name="psum_out", bufs=2))
        ctx.enter_context(tc.manual_schedule())

        gamma_bf = consts.tile([P, HEADS], BF16)
        nc.sync.dma_start(out=gamma_bf[:], in_=gamma.partition_broadcast(P))
        k_raw, q_raw, v_raw = {}, {}, {}
        order = [(h, i) for h in range(HEADS) for i in CHUNK_ORDER]
        first_pieces = (("k", 0), ("q", 3), ("k", 1), ("k", 2), ("k", 3), ("q", 2), ("q", 1), ("q", 0))
        pieces = first_pieces + tuple((kind, i) for i in range(TILES, CHUNKS) for kind in ("k", "q"))
        turns = [(h, pieces[a], pieces[a + 1]) for h in range(HEADS) for a in range(0, len(pieces), 2)]
        groups = [(h, g) for h in range(HEADS) for g in range(CHUNKS)]
        for h, g in groups:
            k_raw[h, g] = raw.tile([P, PACK, P], BF16, name="k_raw_%d_%d" % (h, g))
            q_raw[h, g] = raw.tile([P, TILES, P], BF16, name="q_raw_%d_%d" % (h, g))
            v_raw[h, g] = raw.tile([P, PACK, P], BF16, name="v_raw_%d_%d" % (h, g))

        def load_pieces(j):
            h = turns[j][0]
            for kind, i in turns[j][1:]:
                rows_of_piece = slice(i * GROUP, (i + 1) * GROUP)
                if kind == "k":
                    nc.sync.dma_start(out=k_raw[h, i][:], in_=k[0, h, rows_of_piece, :].rearrange("(p t) d -> p t d", t=PACK))
                else:
                    nc.sync.dma_start(out=q_raw[h, i][:], in_=q[0, h, rows_of_piece, :].rearrange("(c p) d -> p c d", p=P))

        def load_values(j):
            h, g = groups[j]
            nc.sync.dma_start(out=v_raw[h, g][:], in_=v[0, h, g * GROUP : (g + 1) * GROUP, :].rearrange("(p t) d -> p t d", t=PACK))

        for j in range(3):
            load_pieces(j)
        for j in range(2):
            load_values(j)
        load_pieces(3)
        for j in range(2, 4):
            load_values(j)
        for j in range(4, len(turns)):
            load_pieces(j)
            load_values(j)

        identity = consts.tile([P, P], BF16)
        make_identity(nc, identity[:])

        def count(name, width, pattern, base, per_partition):
            numbers = consts.tile([P] + width, F32, name=name)
            nc.gpsimd.iota(numbers[:], pattern=pattern, base=base, channel_multiplier=per_partition,
                           allow_small_or_imprecise_dtypes=True)
            return numbers

        offsets = count("offsets", [P, PACK], [[1, P], [-1, PACK]], 0, 0)
        key_offsets = count("key_offsets", [FLAT * LIVE, PACK], [[-PACK, FLAT * LIVE], [-1, PACK]], 0, 0)
        near_steps = count("near_steps", [TILES + 1], [[P, TILES + 1]], 0, -PACK)
        flat_steps = count("flat_steps", [FLAT], [[P, FLAT]], 0, 1)
        far_steps = count("far_steps", [FAR], [[P, FAR]], 0, 0)
        row_steps = count("row_steps", [PACK], [[-1, PACK]], PACK - 1, 1)
        col_steps = count("col_steps", [1], [[0, 1]], GROUP - PACK + 1, -PACK)
        shift_up = consts.tile([P, 1], F32)
        shift_down = consts.tile([P, 1], F32)
        nc.vector.memset(shift_up[:], SHIFT)
        nc.vector.memset(shift_down[:], -SHIFT)
        warm = consts.tile([P, 1], F32)
        nc.scalar.activation(out=warm[:], in_=shift_down[:], func=ACT.Exp)

        identity_f32 = consts.tile([P, P], F32)
        causal = {}
        for c in range(TILES):
            if c == FLAT:
                make_identity(nc, identity_f32[:])
            flat = c < FLAT
            width = [(c + 1) * LIVE if flat else P, PACK]
            causal[c] = consts.tile([P] + width, F32, name="causal_%d" % c)
            nc.gpsimd.affine_select(out=causal[c][:], in_=key_offsets[:, 0 : (c + 1) * LIVE] if flat else offsets[:],
                                    pattern=[[-PACK, (c + 1) * LIVE], [-1, PACK]] if flat else [[1, P], [-1, PACK]],
                                    compare_op=ALU.is_ge, fill=BEYOND, base=P * c, channel_multiplier=1 if flat else -PACK)


        FLAT_BUFS = 2
        flat_scores = {}
        for c in range(FLAT):
            for b in range(FLAT_BUFS):
                flat_scores[c, b] = consts.tile([P, P, PACK], BF16, name="flat_scores_%d_%d" % (c, b))
                dead = flat_scores[c, b][:, (c + 1) * LIVE : P]
                nc.scalar.activation(out=dead.rearrange("n p t -> n (p t)"), in_=shift_down[:].to_broadcast([P, (P - (c + 1) * LIVE) * PACK]),
                                     func=ACT.Copy, scale=0.0)

        k_turned, q_turned, v_codes, v_scales, v_grouped = {}, {}, {}, {}, {}

        def turn(j):
            h = turns[j][0]
            turned = psum_scalar.tile([P, 2 * PACK, P], BF16, name="turned", tag="for_scalar")
            kept = keep.tile([P, 2 * PACK, P], BF16, name="kq_turned_%d" % j)
            for half, (kind, i) in enumerate(turns[j][1:]):
                piece = k_raw[h, i] if kind == "k" else q_raw[h, i]
                planes = slice(half * PACK, (half + 1) * PACK)
                for a in range(PACK):
                    nc.tensor.transpose(turned[:, half * PACK + a, :], piece[:, a, :], identity[:])
                if kind == "k":
                    k_turned[h, i] = kept[:, planes, :]
                else:
                    q_turned[h, i] = kept[:, planes, :]
            nc.scalar.copy(out=kept[:], in_=turned[:])

        def regroup_values(j):
            h, g = groups[j]
            v_grouped[h, g] = stage.tile([P, P, PACK], BF16, name="v_grouped", align_bytes=64, bufs=4)
            nc.scalar.copy(out=v_grouped[h, g][:].rearrange("p (c a) t -> p c t a", a=RUN),
                           in_=v_raw[h, g][:].rearrange("p t (c a) -> p c t a", a=RUN))

        def quantise_values(j):
            h, g = groups[j]
            v_codes[h, g] = keep.tile([P, P], U32, name="v_codes_%d" % j, align_bytes=64)
            v_scales[h, g] = keep.tile([P, P], U8, name="v_scales_%d" % j, align_bytes=64)
            nc.vector.quantize_mx(
                out=v_codes[h, g][:].bitcast(FP8X4),
                scales=v_scales[h, g][:],
                in_=v_grouped[h, g][:].rearrange("p d t -> p (d t)"),
            )

        y = consts.tile([P, HEADS], F32)
        y_sq = consts.tile([P, HEADS], F32)
        tail = consts.tile([P, HEADS], F32)
        ln_gamma = consts.tile([P, HEADS], F32)
        heads = [slice(h, h + 1) for h in range(HEADS)]
        for h in heads:
            nc.vector.tensor_scalar(out=y[:, h], in0=gamma_bf[:, h], scalar1=-1.0, scalar2=LN_MAX, op0=ALU.add, op1=ALU.min)
        for h in heads:
            nc.vector.tensor_scalar(out=tail[:, h], in0=y[:, h], scalar1=-1.0 / LN_TERMS, scalar2=1.0 / (LN_TERMS - 1),
                                    op0=ALU.mult, op1=ALU.add)
        for h in heads:
            nc.vector.tensor_scalar(out=y_sq[:, h], in0=y[:, h], scalar1=y[:, h], scalar2=None, op0=ALU.mult)
        for term in range(LN_TERMS - 2, 1, -1):
            for h in heads:
                nc.vector.tensor_scalar(out=tail[:, h], in0=tail[:, h], scalar1=y[:, h],
                                        scalar2=1.0 / term if term % 2 else -1.0 / term, op0=ALU.mult, op1=ALU.add)
        for h in heads:
            nc.vector.tensor_scalar(out=ln_gamma[:, h], in0=tail[:, h], scalar1=y_sq[:, h], scalar2=y[:, h],
                                    op0=ALU.mult, op1=ALU.add)

        near_bias, flat_bias, col_bias, near, far, row_fac, col_fac = {}, {}, {}, {}, {}, {}, {}

        def biases(h):
            ln_h = ln_gamma[:, h : h + 1]
            near_bias[h] = consts.tile([P, TILES + 1], F32, name="near_bias_%d" % h)
            flat_bias[h] = consts.tile([P, FLAT], F32, name="flat_bias_%d" % h)
            col_bias[h] = consts.tile([P, 1], F32, name="col_bias_%d" % h)
            far[h] = consts.tile([P, FAR], F32, name="far_%d" % h)
            row_fac[h] = consts.tile([P, PACK], F32, name="row_fac_%d" % h)
            col_fac[h] = consts.tile([P, FAR], F32, name="col_fac_%d" % h)
            for s in [TILES] + list(range(TILES)):
                column = slice(s, s + 1)
                if s < FLAT:
                    nc.vector.tensor_scalar(out=flat_bias[h][:, column], in0=flat_steps[:, column], scalar1=ln_h,
                                            scalar2=None, op0=ALU.mult)
                else:
                    nc.vector.tensor_scalar(out=near_bias[h][:, column], in0=near_steps[:, column], scalar1=ln_h,
                                            scalar2=-SHIFT if s == TILES else 0.0, op0=ALU.mult, op1=ALU.add)
            nc.vector.tensor_scalar(out=col_bias[h][:], in0=col_steps[:], scalar1=ln_h,
                                    scalar2=SHIFT, op0=ALU.mult, op1=ALU.add)

        biases(0)

        def far_factors(h):
            nc.scalar.activation(out=far[h][:], in_=far_steps[:], func=ACT.Exp, scale=ln_gamma[:, h : h + 1], bias=shift_up[:])

        def detour_factors(h):
            ln_h = ln_gamma[:, h : h + 1]
            nc.scalar.activation(out=row_fac[h][:], in_=row_steps[:], func=ACT.Exp, scale=ln_h, bias=shift_down[:])
            nc.scalar.activation(out=col_fac[h][:], in_=far_steps[:], func=ACT.Exp, scale=ln_h, bias=col_bias[h][:])

        def near_table(h, s):
            distance = causal[s] if s < TILES else offsets
            near[h, s] = consts.tile(list(distance.shape), F32, name="near_%d_%d" % (h, s))
            bias = flat_bias[h][:, s : s + 1] if s < FLAT else near_bias[h][:, s : s + 1]
            nc.scalar.activation(out=near[h, s][:], in_=distance[:], func=ACT.Exp, scale=ln_gamma[:, h : h + 1], bias=bias)

        def far_index(i, c, g):
            return TILES * (i - g - 1) + c

        def table_and_number(h, i, c, g):
            if g == i:
                return near[h, c][:], 1.0
            j = far_index(i, c, g)
            return near[h, TILES][:], far[h][:, j : j + 1]

        items = [(h, i, c, g) for h, i in order for c in range(TILES) for g in range(i + 1)]
        units = [items[a : a + UNIT] for a in range(0, len(items), UNIT)]
        last = len(units)

        def live(n):
            return 0 <= n < last

        def is_flat(item):
            h, i, c, g = item
            return g == i and c < FLAT

        def below_diagonal(n):
            return [item for item in units[n] if item[3] < item[1]]

        def helped(n):
            return 0 if n < 1 or len(below_diagonal(n)) < HELPED else HELPED

        def detours(n):
            f = len([item for item in units[n] if is_flat(item)])
            w = 0 if n < 3 else 3 if n == 35 else 2 if n >= 26 and f == 0 or n >= 33 else 1
            return min(w, len(below_diagonal(n)) - helped(n))


        def is_flat(item):
            h, i, c, g = item
            return g == i and c < FLAT

        def arrange(n):
            below = below_diagonal(n)
            flat = [item for item in units[n] if is_flat(item)]
            diagonal = [item for item in units[n] if item[3] == item[1] and not is_flat(item)]
            taken = detours(n) + helped(n)
            if n == 0:
                below = sorted(below, key=lambda item: item[3])
                return below[:4] + flat + below[4:] + diagonal
            return below[:taken] + flat + below[taken:] + diagonal

        slot_items = [arrange(n) for n in range(last)]
        direct_items = [(n, slot) for n in range(last) for slot in range(detours(n) + helped(n), UNIT)]
        first_direct = [direct_items.index((n, detours(n) + helped(n))) for n in range(last)]
        flat_items = [(n, slot) for n, slot in direct_items if is_flat(slot_items[n][slot])]

        banks, scaled, wide, rows, back, grouped, codes, scales, sums = {}, {}, {}, {}, {}, {}, {}, {}, {}

        def keys_on_partitions(pool, tag, h, i, c, g):
            bank = pool.tile([P, PACK, P], F32, name="bank", tag=tag)
            for t in range(PACK):
                nc.tensor.matmul(out=bank[:, t, :], lhsT=k_turned[h, g][:, t, :], rhs=q_turned[h, i][:, c, :],
                                 start=True, stop=True)
            return bank

        def queries_on_partitions(pool, tag, keys, h, i, c, g):
            bank = pool.tile([P, PACK * P], F32, name="bank", tag=tag)
            view = bank[:, 0 : PACK * keys].rearrange("n (t p) -> n t p", t=PACK)
            nc.tensor.matmul(out=view, lhsT=q_turned[h, i][:, c, :], rhs=k_turned[h, g][:, :, 0:keys], start=True, stop=True)
            return view

        def direct_scores(position):
            if position < len(direct_items):
                n, slot = direct_items[position]
                item = slot_items[n][slot]
                if is_flat(item):
                    view = queries_on_partitions(psum_vector, "for_vector", (item[2] + 1) * LIVE, *item)
                    banks[n, slot] = view.rearrange("n t p -> n p t")
                else:
                    bank = keys_on_partitions(psum_vector, "for_vector", *item)
                    banks[n, slot] = bank[:].rearrange("p t n -> p n t")

        def flat_tile(n, slot):
            c = slot_items[n][slot][2]
            turn_number = [pair for pair in flat_items if slot_items[pair[0]][pair[1]][2] == c].index((n, slot))
            return flat_scores[c, turn_number % FLAT_BUFS]

        def direct_step(n, r):
            if live(n) and detours(n) + helped(n) + r < UNIT:
                slot = detours(n) + helped(n) + r
                item = slot_items[n][slot]
                table, number = table_and_number(*item)
                if is_flat(item):
                    target = flat_tile(n, slot)[:, 0 : (item[2] + 1) * LIVE]
                else:
                    target = grouped[n][:, slot]
                nc.vector.scalar_tensor_tensor(out=target, in0=banks[n, slot], scalar=number, in1=table, op0=ALU.mult, op1=ALU.mult)
                direct_scores(first_direct[n] + r + DIRECT_BANKS)

        def flat_turn(n):
            if live(n):
                for slot in range(UNIT):
                    if is_flat(slot_items[n][slot]):
                        turned = psum_scalar.tile([P, PAIRS, P], F32, name="flat_turned", tag="for_scalar")
                        words = flat_tile(n, slot)[:].rearrange("n p t -> n (p t)").bitcast(F32)
                        for u in range(PAIRS):
                            nc.tensor.transpose(turned[:, u, :], words[:, u : PAIRS * P : PAIRS], identity_f32[:])
                        target = grouped[n][:, slot].rearrange("p n t -> p (n t)").bitcast(F32)
                        nc.scalar.copy(out=target.rearrange("p (n u) -> p n u", u=PAIRS), in_=turned[:].rearrange("p u n -> p n u"))

        def helped_scores(n, r):
            if live(n) and r < helped(n):
                slot = detours(n) + r
                table, number = table_and_number(*slot_items[n][slot])
                bank = keys_on_partitions(psum_scalar, "for_scalar", *slot_items[n][slot])
                if r == 0:
                    scaled[n] = stage.tile([P, HELPED, P, PACK], F32, name="scaled", bufs=3)
                nc.scalar.activation(out=scaled[n][:, r], in_=bank[:].rearrange("p t n -> p n t"),
                                     func=ACT.Copy, scale=number)

        def helped_mask(n):
            if live(n) and helped(n):
                slot = detours(n)
                table, number = table_and_number(*slot_items[n][slot])
                nc.gpsimd.tensor_tensor(out=grouped[n][:, slot : slot + HELPED], in0=scaled[n][:],
                                        in1=table.unsqueeze(1).to_broadcast([P, HELPED, P, PACK]), op=ALU.mult)

        def detour_out(n, r):
            if live(n) and r < detours(n):
                h, i, c, g = slot_items[n][r]
                wide[n, r] = queries_on_partitions(psum_scalar, "for_scalar", P, h, i, c, g)
                rows[n, r] = stage.tile([P, PACK, P], F32, name="rows", bufs=6)
                for t in range(PACK):
                    nc.scalar.activation(out=rows[n, r][:, t, :], in_=wide[n, r][:, t, :], func=ACT.Copy,
                                         scale=row_fac[h][:, t : t + 1])

        def detour_back(n, r):
            if live(n) and r < detours(n):
                h, i, c, g = slot_items[n][r]
                j = far_index(i, c, g)
                back[n, r] = psum_scalar.tile([P, PACK, P], F32, name="back", tag="for_scalar")
                for t in range(PACK):
                    nc.tensor.transpose(back[n, r][:, t, :], rows[n, r][:, t, :], identity_f32[:])
                nc.scalar.activation(out=grouped[n][:, r], in_=back[n, r][:].rearrange("p t n -> p n t"),
                                     func=ACT.Copy, scale=col_fac[h][:, j : j + 1])

        def quantise_scores(n, begin=0, end=UNIT):
            if live(n):
                if begin == 0:
                    codes[n] = packed.tile([P, UNIT * P], U32, name="codes", align_bytes=64)
                    scales[n] = packed.tile([P, UNIT * P], U8, name="scales", align_bytes=64)
                cols = slice(begin * P, end * P)
                nc.vector.quantize_mx(out=codes[n][:, cols].bitcast(FP8X4), scales=scales[n][:, cols],
                                      in_=grouped[n][:, begin:end].rearrange("p s n t -> p (s n t)"))

        store_after = {chunk: {TILES - 1: 0} for chunk in order}
        store_after[order[-1]] = {TILES - 2: 0, TILES - 1: TILES - 1}

        def attend(n):
            if live(n):
                for item in units[n]:
                    h, i, c, g = item
                    slot = slot_items[n].index(item)
                    if c == 0 and g == 0:
                        sums[h, i] = psum_out.tile([P, TILES, P], F32, name="sums")
                    cols = slice(slot * P, (slot + 1) * P)
                    nc.tensor.matmul_mx(out=sums[h, i][:, c, :],
                                        lhsT=codes[n][:, cols].bitcast(FP8X4), lhsT_scale=scales[n][:, cols],
                                        rhs=v_codes[h, g][:].bitcast(FP8X4), rhs_scale=v_scales[h, g][:],
                                        start=(g == 0), stop=(g == i))
                    if g == i and c in store_after[h, i]:
                        begin = store_after[h, i].get(c)
                        tiles = slice(begin, c + 1)
                        result = results.tile([P, TILES, P], F32)
                        nc.scalar.copy(out=result[:, tiles], in_=sums[h, i][:, tiles])
                        rows_of_tiles = slice(i * GROUP + begin * P, i * GROUP + (c + 1) * P)
                        nc.sync.dma_start(out=out[0, h, rows_of_tiles, :].rearrange("(c p) d -> p c d", p=P), in_=result[:, tiles])

        def turn_step(j):
            return 2 * j - 6

        def regroup_step(j):
            return max(turn_step(j), j // 2)

        def prepare(n):
            for j in range(len(turns)):
                if j > 3 and n == turn_step(j):
                    turn(j)
                if n == regroup_step(j):
                    regroup_values(j)
            if n == 4:
                biases(1)
            if n == 5:
                far_factors(1)
                detour_factors(1)
            if n >= 5 and n % 2 == 1 and (n - 5) // 2 <= TILES:
                near_table(1, (n - 5) // 2)

        def quantise_prepared(n):
            for j in range(len(turns)):
                if n == regroup_step(j) + 2:
                    quantise_values(j)

        turn(0)
        far_factors(0)
        near_table(0, TILES)
        direct_scores(0)
        turn(1)
        direct_scores(1)
        direct_scores(2)
        grouped[0] = stage.tile([P, UNIT, P, PACK], BF16, name="grouped", align_bytes=64)
        turn(2)
        direct_step(0, 0)
        direct_step(0, 1)
        for s in range(FLAT):
            near_table(0, s)
        direct_step(0, 2)
        helped_scores(1, 0)
        direct_step(0, 3)
        helped_scores(1, 1)
        direct_step(0, 4)
        direct_step(0, 5)
        flat_turn(0)
        near_table(0, 2)
        near_table(0, 3)
        prepare(0)
        grouped[1] = stage.tile([P, UNIT, P, PACK], BF16, name="grouped", align_bytes=64)
        helped_mask(1)
        detour_factors(0)
        detour_out(2, 0)
        helped_scores(2, 0)
        helped_scores(2, 1)
        direct_step(0, 6)
        direct_step(0, 7)
        turn(3)
        for n in range(1, last + 2):
            helped_scores(n + 2, 0)
            direct_step(n, 0)
            helped_scores(n + 2, 1)
            direct_step(n, 1)
            quantise_prepared(n)
            if n < last:
                quantise_scores(n - 1)
            if live(n + 1):
                grouped[n + 1] = stage.tile([P, UNIT, P, PACK], BF16, name="grouped", align_bytes=64)
            helped_mask(n + 1)
            detour_out(n + 2, 0)
            for m in range(last):
                if n == max(m + 2, 3):
                    attend(m)
            flat_turn(n)
            direct_step(n, 2)
            detour_back(n + 1, 0)
            if live(n + 2):
                for r in range(1, detours(n + 2)):
                    detour_out(n + 2, r)
            direct_step(n, 3)
            if n == last - 1:
                quantise_scores(n, 0, UNIT // 2)
            if live(n + 1):
                for r in range(1, detours(n + 1)):
                    detour_back(n + 1, r)
            prepare(n)
            direct_step(n, 4)
            direct_step(n, 5)
            if n == last - 1:
                quantise_scores(n, UNIT // 2, UNIT)
